import numpy as np
import ml_dtypes


def mxq(x, axis, fmt="e4m3"):
    dtype, down = {"e4m3": (ml_dtypes.float8_e4m3fn, 7), "e5m2": (ml_dtypes.float8_e5m2, 14)}[fmt]
    v = np.moveaxis(np.asarray(x, np.float32).astype(ml_dtypes.bfloat16).astype(np.float64), axis, -1)
    blocks = v.reshape(v.shape[:-1] + (-1, 32))
    amax = np.abs(blocks).max(-1, keepdims=True)
    byte = np.maximum(np.where(amax > 0, np.frexp(amax)[1] - 1 + 127, 0) - down, 1)
    scale = np.exp2(byte - 127.0)
    codes = (blocks / scale).astype(np.float32).astype(dtype).astype(np.float64)
    return np.moveaxis((codes * scale).reshape(v.shape), -1, axis)


WIDE = False


def mx_kscale(k):
    if not WIDE:
        return np.ones(k)
    levels = np.array([10, -10, 5, -5, 0])
    a = np.random.permutation(np.resize(levels, k // 512 * 4)).reshape(k // 512, 4)
    idx = np.arange(k)
    return np.exp2(a[idx // 512, idx % 128 // 32])


BF16 = ml_dtypes.bfloat16


def bf(x):
    return np.asarray(x, np.float32).astype(BF16)


def f64(x):
    return np.asarray(x).astype(np.float64)


E2M1 = np.array([0.0, 0.5, 1.0, 1.5, 2.0, 3.0, 4.0, 6.0, -0.0, -0.5, -1.0, -1.5, -2.0, -3.0, -4.0, -6.0])


def pack_weight(w, fmt):
    k, n = w.shape
    w = f64(bf(w)).reshape(k // 32, 32, n)
    amax = np.abs(w).max(1)
    if fmt == "e4m3":
        byte = np.frexp(amax)[1] - 1 + 127 - 7
    else:
        mant, ex = np.frexp(amax / 6.0)
        byte = np.where(mant > 0.5, ex, ex - 1) + 127
    byte = np.clip(np.where(amax > 0, byte, 1), 1, 254)
    scaled = (w * np.exp2(127.0 - byte)[:, None, :]).reshape(k, n).astype(np.float32)
    by_word = np.ascontiguousarray(scaled.reshape(k // 512, 128, 4, n).transpose(0, 1, 3, 2))
    if fmt == "e4m3":
        words = by_word.astype(ml_dtypes.float8_e4m3fn).view(np.uint8)
    else:
        c = by_word.astype(ml_dtypes.float4_e2m1fn).view(np.uint8) & 0xF
        words = c[..., 0::2] | (c[..., 1::2] << 4)
    return np.ascontiguousarray(words), np.ascontiguousarray(byte.astype(np.uint8).reshape(k // 512, 16, n))


def unpack_weight(words, scales, fmt):
    g, p, n, _ = words.shape
    if fmt == "e4m3":
        vals = np.ascontiguousarray(words).view(ml_dtypes.float8_e4m3fn).astype(np.float64)
    else:
        nib = np.empty((g, p, n, 4), np.uint8)
        nib[..., 0::2] = words & 0xF
        nib[..., 1::2] = words >> 4
        vals = E2M1[nib]
    vals = vals * np.repeat(np.exp2(scales.astype(np.float64) - 127.0), 8, axis=1)[..., None]
    return vals.transpose(0, 1, 3, 2).reshape(g * 512, n)


B, IN, M, OUT = 1024, 1024, 512, 512
F = 2 * M
EPS = 1e-12
FMT = "e4m3"


def setup_inputs():
    s, t = mx_kscale(IN), mx_kscale(F)
    x = bf(np.random.standard_normal((B, IN)) * s)
    W1_words, W1_scales = pack_weight(np.random.standard_normal((IN, F)) / np.sqrt(IN) / s[:, None] * t, FMT)
    b1 = bf(np.random.standard_normal(F) * 0.1 * t)
    W2_words, W2_scales = pack_weight(np.random.standard_normal((F, M)) / np.sqrt(F) / t[:, None], FMT)
    b2 = bf(np.random.standard_normal(M) * 0.3)
    return {"x": x,
            "W1_words": W1_words,
            "W1_scales": W1_scales,
            "b1": b1,
            "W2_words": W2_words,
            "W2_scales": W2_scales,
            "b2": b2}


def reference(x, W1_words, W1_scales, b1, W2_words, W2_scales, b2):
    h = np.maximum((mxq(f64(x), 1, "e4m3") @ unpack_weight(W1_words, W1_scales, FMT)) + f64(b1), 0.0)
    v = (mxq(h, 1, "e4m3") @ unpack_weight(W2_words, W2_scales, FMT)) + f64(b2)
    norm = np.sqrt(np.sum(v * v, axis=-1, keepdims=True))
    return v / np.maximum(norm, EPS)

@@ -1,0 +1,248 @@
+from contextlib import ExitStack
+
+import concourse.masks as masks
+import concourse.mybir as mybir
+
+F32 = mybir.dt.float32
+BF16 = mybir.dt.bfloat16
+I32 = mybir.dt.int32
+U32 = mybir.dt.uint32
+U8 = mybir.dt.uint8
+FP8X4 = mybir.dt.float8_e4m3fn_x4
+ALU = mybir.AluOpType
+ACT = mybir.ActivationFunctionType
+
+P = 128
+BATCH = 1024
+K_PASS = 512
+PASSES = 2
+HIDDEN = 1024
+OUT = 512
+BANK = 512
+ROW_TILES = BATCH // P
+HIDDEN_BANKS = HIDDEN // BANK
+QUADRANTS = 4
+EPS = 1e-12
+
+FLOPS = 2 * BATCH * (PASSES * K_PASS) * HIDDEN + 2 * BATCH * HIDDEN * OUT
+
+
+def tile_geometricmanifoldnetwork_pa_kernel(
+    tc, x, W1_words, W1_scales, b1, W2_words, W2_scales, b2, out
+):
+    nc = tc.nc
+    with ExitStack() as ctx:
+        consts = ctx.enter_context(tc.tile_pool(name="consts", bufs=1))
+        x_pool = ctx.enter_context(tc.tile_pool(name="x_pool", bufs=ROW_TILES))
+        work = ctx.enter_context(tc.tile_pool(name="work", bufs=3))
+        psum = ctx.enter_context(tc.psum_pool(name="psum", bufs=1))
+        ctx.enter_context(tc.manual_schedule())
+
+        w1_scales = consts.tile([P, PASSES, HIDDEN], U8, align_bytes=64)
+        w2_scales = consts.tile([P, PASSES, OUT], U8, align_bytes=64)
+        nc.vector.memset(w1_scales[:].bitcast(I32), 0)
+        bias_rows = consts.tile([P, HIDDEN + OUT], BF16)
+        nc.vector.memset(bias_rows[:], 0.0)
+        ones = consts.tile([P, P], BF16)
+        nc.vector.memset(ones[:], 1.0)
+        nc.vector.memset(w2_scales[:].bitcast(I32), 0)
+        minus_half = consts.tile([P, 1], F32)
+        nc.vector.memset(minus_half[:], -0.5)
+        identity = consts.tile([P, P], F32)
+        masks.make_identity(nc, identity[:])
+
+        nc.scalar.dma_start(out=bias_rows[0:1, 0:HIDDEN], in_=b1.unsqueeze(0))
+        nc.scalar.dma_start(out=bias_rows[0:1, HIDDEN : HIDDEN + OUT], in_=b2.unsqueeze(0))
+
+        x_tiles = []
+
+        def load_x(i):
+            x_tile = x_pool.tile([P, PASSES * K_PASS], BF16)
+            nc.sync.dma_start(out=x_tile[:], in_=x[i * P : (i + 1) * P, :])
+            x_tiles.append(x_tile)
+
+        def load_scales(plane, scales):
+            for q in range(QUADRANTS):
+                nc.sync.dma_start(
+                    out=plane[32 * q : 32 * q + 4].bitcast(I32),
+                    in_=scales[:, 4 * q : 4 * q + 4, :].bitcast(I32).rearrange("g r n -> r g n"),
+                )
+
+        load_x(0)
+        load_x(1)
+        load_scales(w1_scales, W1_scales)
+        w1_bytes = W1_words.rearrange("g p n t -> p g (n t)")
+        w1_words = []
+        for j in range(HIDDEN_BANKS):
+            w1_part = consts.tile([P, PASSES, BANK], U32, align_bytes=64, name="w1_part%d" % j)
+            nc.sync.dma_start(
+                out=w1_part[:].bitcast(I32),
+                in_=w1_bytes[:, :, 4 * BANK * j : 4 * BANK * (j + 1)].bitcast(I32),
+            )
+            w1_words.append(w1_part)
+        load_x(2)
+        load_x(3)
+        load_scales(w2_scales, W2_scales)
+        w2_words = consts.tile([P, PASSES, OUT], U32, align_bytes=64)
+        nc.sync.dma_start(
+            out=w2_words[:].bitcast(I32),
+            in_=W2_words.rearrange("g p n t -> p g (n t)").bitcast(I32),
+        )
+        for i in range(4, ROW_TILES):
+            load_x(i)
+
+        b1_sorted = consts.tile([P, HIDDEN_BANKS, 2, P, 2], F32)
+        b2_spread = consts.tile([P, OUT], F32)
+
+        def spread_biases():
+            for j in range(HIDDEN_BANKS):
+                spread = psum.tile([P, BANK], F32, tag="h_acc", bufs=4)
+                nc.tensor.matmul(
+                    out=spread[:],
+                    lhsT=ones[:],
+                    rhs=bias_rows[:, j * BANK : (j + 1) * BANK],
+                    start=True,
+                    stop=True,
+                )
+                nc.scalar.copy(
+                    out=b1_sorted[:, j],
+                    in_=spread[:].rearrange("r (p u e) -> r u p e", u=2, e=2),
+                )
+            spread = psum.tile([P, BANK], F32, tag="h_acc", bufs=4)
+            nc.tensor.matmul(
+                out=spread[:],
+                lhsT=ones[:],
+                rhs=bias_rows[:, HIDDEN : HIDDEN + OUT],
+                start=True,
+                stop=True,
+            )
+            nc.scalar.copy(out=b2_spread[:], in_=spread[:])
+
+        x_mx = {}
+        h_acc = {}
+        h_sorted = {}
+        h_grouped = {}
+        h_mx = {}
+        v_acc = {}
+        v_rows = {}
+        x_grouped = {}
+
+        def transpose_x(i):
+            words = x_tiles[i][:].bitcast(F32)
+            x_t = psum.tile([P, PASSES, 2, P], F32)
+            for g in range(PASSES):
+                for u in range(2):
+                    nc.tensor.transpose(
+                        x_t[:, g, u, :], words[:, 256 * g + u : 256 * (g + 1) : 2], identity[:]
+                    )
+            grouped = work.tile([P, PASSES * K_PASS], BF16, align_bytes=64, tag="x_grouped")
+            nc.scalar.copy(
+                out=grouped[:].bitcast(F32).rearrange("p (g r u) -> p g r u", g=PASSES, u=2),
+                in_=x_t[:].rearrange("p g u r -> p g r u"),
+            )
+            x_grouped[i] = grouped
+
+        def quantise(grouped, tag):
+            codes = work.tile([P, PASSES * P], U32, align_bytes=64, tag=tag + "_codes")
+            plane = work.tile([P, PASSES * P], U8, align_bytes=64, tag=tag + "_plane")
+            nc.vector.quantize_mx(out=codes[:].bitcast(FP8X4), scales=plane[:], in_=grouped[:])
+            return codes, plane
+
+        def multiply(acc, rows_mx, words, scales):
+            codes, plane = rows_mx
+            for g in range(PASSES):
+                nc.tensor.matmul_mx(
+                    out=acc[:],
+                    lhsT=codes[:, g * P : (g + 1) * P].bitcast(FP8X4),
+                    lhsT_scale=plane[:, g * P : (g + 1) * P],
+                    rhs=words[:, g, :].bitcast(FP8X4),
+                    rhs_scale=scales[:, g, :],
+                    start=(g == 0),
+                    stop=(g == PASSES - 1),
+                )
+
+        def multiply_w1(i):
+            h_acc[i] = []
+            for j in range(HIDDEN_BANKS):
+                acc = psum.tile([P, BANK], F32, tag="h_acc", bufs=4)
+                multiply(acc, x_mx[i], w1_words[j], w1_scales[:, :, j * BANK : (j + 1) * BANK])
+                h_acc[i].append(acc)
+
+        def add_b1(i):
+            biased = work.tile([P, HIDDEN_BANKS, 2, P, 2], BF16, tag="h_sorted")
+            for j in range(HIDDEN_BANKS):
+                nc.vector.tensor_tensor(
+                    out=biased[:, j],
+                    in0=h_acc[i][j][:].rearrange("r (p u e) -> r u p e", u=2, e=2),
+                    in1=b1_sorted[:, j],
+                    op=ALU.add,
+                )
+            h_sorted[i] = biased
+
+        def transpose_h(i):
+            words = h_sorted[i][:].rearrange("r g u p e -> r (g u p e)").bitcast(F32)
+            h_t = psum.tile([P, PASSES, 2, P], F32)
+            for g in range(PASSES):
+                for u in range(2):
+                    first = (2 * g + u) * P
+                    nc.tensor.transpose(h_t[:, g, u, :], words[:, first : first + P], identity[:])
+            grouped = work.tile([P, PASSES * K_PASS], BF16, align_bytes=64, tag="h_grouped")
+            for g in range(PASSES):
+                nc.scalar.activation(
+                    out=grouped[:, g * K_PASS : (g + 1) * K_PASS].rearrange(
+                        "p (r u e) -> p r u e", u=2, e=2
+                    ),
+                    in_=h_t[:, g].bitcast(BF16).rearrange("p u (r e) -> p r u e", e=2),
+                    func=ACT.Relu,
+                )
+            h_grouped[i] = grouped
+
+        def multiply_w2(i):
+            acc = psum.tile([P, OUT], F32, tag="v_acc", bufs=2)
+            multiply(acc, h_mx[i], w2_words, w2_scales)
+            v_acc[i] = acc
+
+        def add_b2(i):
+            v = work.tile([P, OUT], F32, tag="v")
+            nc.vector.tensor_tensor(out=v[:], in0=v_acc[i][:], in1=b2_spread[:], op=ALU.add)
+            v_rows[i] = v
+
+        def normalise_and_store(i):
+            v = v_rows[i]
+            squares = work.tile([P, OUT], BF16, tag="squares")
+            norm2 = work.tile([P, 1], F32, tag="norm2")
+            nc.scalar.activation(out=squares[:], in_=v[:], func=ACT.Square, accum_out=norm2[:])
+            floored = work.tile([P, 1], F32, tag="floored")
+            nc.gpsimd.tensor_scalar(
+                out=floored[:], in0=norm2[:], scalar1=EPS * EPS, scalar2=None, op0=ALU.max
+            )
+            inverse = work.tile([P, 1], F32, tag="inverse")
+            nc.gpsimd.tensor_tensor(out=inverse[:], in0=floored[:], in1=minus_half[:], op=ALU.pow)
+            unit = work.tile([P, OUT], F32, tag="unit")
+            nc.gpsimd.tensor_scalar(
+                out=unit[:], in0=v[:], scalar1=inverse[:, 0:1], scalar2=0.0, op0=ALU.mult, op1=ALU.add
+            )
+            nc.sync.dma_start(out=out[i * P : (i + 1) * P, :], in_=unit[:])
+
+        def live(i):
+            return 0 <= i < ROW_TILES
+
+        for r in range(ROW_TILES + 4):
+            if live(r):
+                transpose_x(r)
+            if r == 0:
+                spread_biases()
+            if live(r - 2):
+                transpose_h(r - 2)
+            if live(r):
+                x_mx[r] = quantise(x_grouped[r], "x")
+            if live(r - 1):
+                multiply_w1(r - 1)
+                add_b1(r - 1)
+            if live(r - 2):
+                h_mx[r - 2] = quantise(h_grouped[r - 2], "h")
+            if live(r - 3):
+                multiply_w2(r - 3)
+                add_b2(r - 3)
+            if live(r - 4):
+                normalise_and_store(r - 4)

@@ -41,7 +41,7 @@ def tile_geometricmanifoldnetwork_pa_kernel(
         w1_scales = consts.tile([P, PASSES, HIDDEN], U8, align_bytes=64)
         w2_scales = consts.tile([P, PASSES, OUT], U8, align_bytes=64)
         nc.vector.memset(w1_scales[:].bitcast(I32), 0)
-        bias_rows = consts.tile([P, HIDDEN + OUT], BF16)
+        bias_rows = consts.tile([P, HIDDEN], BF16)
         nc.vector.memset(bias_rows[:], 0.0)
         ones = consts.tile([P, P], BF16)
         nc.vector.memset(ones[:], 1.0)
@@ -51,8 +51,7 @@ def tile_geometricmanifoldnetwork_pa_kernel(
         identity = consts.tile([P, P], F32)
         masks.make_identity(nc, identity[:])
 
-        nc.scalar.dma_start(out=bias_rows[0:1, 0:HIDDEN], in_=b1.unsqueeze(0))
-        nc.scalar.dma_start(out=bias_rows[0:1, HIDDEN : HIDDEN + OUT], in_=b2.unsqueeze(0))
+        nc.scalar.dma_start(out=bias_rows[0:1, :], in_=b1.unsqueeze(0))
 
         x_tiles = []
 
@@ -90,11 +89,12 @@ def tile_geometricmanifoldnetwork_pa_kernel(
         )
         for i in range(4, ROW_TILES):
             load_x(i)
+        b2_spread = consts.tile([P, OUT], BF16)
+        nc.sync.dma_start(out=b2_spread[:], in_=b2.partition_broadcast(P))
 
         b1_sorted = consts.tile([P, HIDDEN_BANKS, 2, P, 2], F32)
-        b2_spread = consts.tile([P, OUT], F32)
 
-        def spread_biases():
+        def spread_b1():
             for j in range(HIDDEN_BANKS):
                 spread = psum.tile([P, BANK], F32, tag="h_acc", bufs=4)
                 nc.tensor.matmul(
@@ -108,15 +108,6 @@ def tile_geometricmanifoldnetwork_pa_kernel(
                     out=b1_sorted[:, j],
                     in_=spread[:].rearrange("r (p u e) -> r u p e", u=2, e=2),
                 )
-            spread = psum.tile([P, BANK], F32, tag="h_acc", bufs=4)
-            nc.tensor.matmul(
-                out=spread[:],
-                lhsT=ones[:],
-                rhs=bias_rows[:, HIDDEN : HIDDEN + OUT],
-                start=True,
-                stop=True,
-            )
-            nc.scalar.copy(out=b2_spread[:], in_=spread[:])
 
         x_mx = {}
         h_acc = {}
@@ -129,7 +120,7 @@ def tile_geometricmanifoldnetwork_pa_kernel(
 
         def transpose_x(i):
             words = x_tiles[i][:].bitcast(F32)
-            x_t = psum.tile([P, PASSES, 2, P], F32)
+            x_t = psum.tile([P, PASSES, 2, P], F32, tag="transposed", bufs=2)
             for g in range(PASSES):
                 for u in range(2):
                     nc.tensor.transpose(
@@ -181,20 +172,19 @@ def tile_geometricmanifoldnetwork_pa_kernel(
 
         def transpose_h(i):
             words = h_sorted[i][:].rearrange("r g u p e -> r (g u p e)").bitcast(F32)
-            h_t = psum.tile([P, PASSES, 2, P], F32)
+            h_t = psum.tile([P, 2, PASSES, P], F32, tag="transposed", bufs=2)
             for g in range(PASSES):
                 for u in range(2):
                     first = (2 * g + u) * P
-                    nc.tensor.transpose(h_t[:, g, u, :], words[:, first : first + P], identity[:])
+                    nc.tensor.transpose(h_t[:, u, g, :], words[:, first : first + P], identity[:])
             grouped = work.tile([P, PASSES * K_PASS], BF16, align_bytes=64, tag="h_grouped")
-            for g in range(PASSES):
-                nc.scalar.activation(
-                    out=grouped[:, g * K_PASS : (g + 1) * K_PASS].rearrange(
-                        "p (r u e) -> p r u e", u=2, e=2
-                    ),
-                    in_=h_t[:, g].bitcast(BF16).rearrange("p u (r e) -> p r u e", e=2),
-                    func=ACT.Relu,
-                )
+            nc.scalar.activation(
+                out=grouped[:].rearrange("p (c u e) -> p c u e", u=2, e=2),
+                in_=h_t[:].rearrange("p u g r -> p u (g r)").bitcast(BF16).rearrange(
+                    "p u (c e) -> p c u e", e=2
+                ),
+                func=ACT.Relu,
+            )
             h_grouped[i] = grouped
 
         def multiply_w2(i):
@@ -227,22 +217,26 @@ def tile_geometricmanifoldnetwork_pa_kernel(
         def live(i):
             return 0 <= i < ROW_TILES
 
-        for r in range(ROW_TILES + 4):
-            if live(r):
-                transpose_x(r)
-            if r == 0:
-                spread_biases()
-            if live(r - 2):
-                transpose_h(r - 2)
-            if live(r):
-                x_mx[r] = quantise(x_grouped[r], "x")
-            if live(r - 1):
-                multiply_w1(r - 1)
-                add_b1(r - 1)
-            if live(r - 2):
-                h_mx[r - 2] = quantise(h_grouped[r - 2], "h")
-            if live(r - 3):
-                multiply_w2(r - 3)
-                add_b2(r - 3)
-            if live(r - 4):
-                normalise_and_store(r - 4)
+        transpose_x(0)
+        transpose_x(1)
+        spread_b1()
+        x_mx[0] = quantise(x_grouped[0], "x")
+        for n in range(ROW_TILES + 3):
+            if live(n):
+                multiply_w1(n)
+            if live(n - 3):
+                multiply_w2(n - 3)
+            if live(n + 1):
+                x_mx[n + 1] = quantise(x_grouped[n + 1], "x")
+            if live(n):
+                add_b1(n)
+            if live(n - 2):
+                h_mx[n - 2] = quantise(h_grouped[n - 2], "h")
+            if live(n - 3):
+                add_b2(n - 3)
+            if live(n + 2):
+                transpose_x(n + 2)
+            if live(n - 1):
+                transpose_h(n - 1)
+            if live(n - 3):
+                normalise_and_store(n - 3)

@@ -16,11 +16,14 @@ P = 128
 BATCH = 1024
 K_PASS = 512
 PASSES = 2
+PACK = 4
 HIDDEN = 1024
 OUT = 512
 BANK = 512
 ROW_TILES = BATCH // P
-HIDDEN_BANKS = HIDDEN // BANK
+BLOCK = 512
+BLOCKS = BATCH // BLOCK
+TILES_IN_BLOCK = BLOCK // P
 QUADRANTS = 4
 EPS = 1e-12
 
@@ -34,31 +37,27 @@ def tile_geometricmanifoldnetwork_pa_kernel(
     with ExitStack() as ctx:
         consts = ctx.enter_context(tc.tile_pool(name="consts", bufs=1))
         x_pool = ctx.enter_context(tc.tile_pool(name="x_pool", bufs=ROW_TILES))
-        work = ctx.enter_context(tc.tile_pool(name="work", bufs=3))
-        psum = ctx.enter_context(tc.psum_pool(name="psum", bufs=1))
+        blocks = ctx.enter_context(tc.tile_pool(name="blocks", bufs=BLOCKS))
+        halves = ctx.enter_context(tc.tile_pool(name="halves", bufs=BLOCKS * PASSES))
+        work = ctx.enter_context(tc.tile_pool(name="work", bufs=ROW_TILES))
+        psum = ctx.enter_context(tc.psum_pool(name="psum", bufs=8))
         ctx.enter_context(tc.manual_schedule())
 
-        w1_scales = consts.tile([P, PASSES, HIDDEN], U8, align_bytes=64)
+        w1_scales_raw = consts.tile([P, PASSES * HIDDEN], U8, align_bytes=64)
         w2_scales = consts.tile([P, PASSES, OUT], U8, align_bytes=64)
-        nc.vector.memset(w1_scales[:].bitcast(I32), 0)
-        bias_rows = consts.tile([P, HIDDEN], BF16)
-        nc.vector.memset(bias_rows[:], 0.0)
-        ones = consts.tile([P, P], BF16)
-        nc.vector.memset(ones[:], 1.0)
+        nc.vector.memset(w1_scales_raw[:].bitcast(I32), 0)
         nc.vector.memset(w2_scales[:].bitcast(I32), 0)
         minus_half = consts.tile([P, 1], F32)
         nc.vector.memset(minus_half[:], -0.5)
+        warm = consts.tile([P, 1], F32)
+        nc.scalar.activation(out=warm[:], in_=minus_half[:], func=ACT.Relu)
         identity = consts.tile([P, P], F32)
         masks.make_identity(nc, identity[:])
 
-        nc.scalar.dma_start(out=bias_rows[0:1, :], in_=b1.unsqueeze(0))
-
-        x_tiles = []
-
-        def load_x(i):
-            x_tile = x_pool.tile([P, PASSES * K_PASS], BF16)
-            nc.sync.dma_start(out=x_tile[:], in_=x[i * P : (i + 1) * P, :])
-            x_tiles.append(x_tile)
+        b1_bf = consts.tile([P, PASSES, PACK], BF16)
+        nc.scalar.dma_start(out=b1_bf[:], in_=b1.rearrange("(c p t) -> p c t", c=PASSES, t=PACK))
+        b1_cols = consts.tile([P, PASSES, PACK], F32)
+        nc.gpsimd.tensor_copy(out=b1_cols[:], in_=b1_bf[:])
 
         def load_scales(plane, scales):
             for q in range(QUADRANTS):
@@ -67,137 +66,147 @@ def tile_geometricmanifoldnetwork_pa_kernel(
                     in_=scales[:, 4 * q : 4 * q + 4, :].bitcast(I32).rearrange("g r n -> r g n"),
                 )
 
-        load_x(0)
-        load_x(1)
-        load_scales(w1_scales, W1_scales)
+        x_tiles = []
+        for i in range(ROW_TILES):
+            x_tile = x_pool.tile([P, PASSES * K_PASS], BF16)
+            nc.sync.dma_start(out=x_tile[:], in_=x[i * P : (i + 1) * P, :])
+            x_tiles.append(x_tile)
+            if i == 0:
+                load_scales(w1_scales_raw[:].rearrange("p (g n) -> p g n", g=PASSES), W1_scales)
         w1_bytes = W1_words.rearrange("g p n t -> p g (n t)")
-        w1_words = []
-        for j in range(HIDDEN_BANKS):
-            w1_part = consts.tile([P, PASSES, BANK], U32, align_bytes=64, name="w1_part%d" % j)
+        w1_raw = []
+        for c in range(PASSES):
+            w1_part = consts.tile([P, PASSES, K_PASS], I32, align_bytes=64, name="w1_part%d" % c)
             nc.sync.dma_start(
-                out=w1_part[:].bitcast(I32),
-                in_=w1_bytes[:, :, 4 * BANK * j : 4 * BANK * (j + 1)].bitcast(I32),
+                out=w1_part[:],
+                in_=w1_bytes[:, :, 4 * K_PASS * c : 4 * K_PASS * (c + 1)].bitcast(I32),
             )
-            w1_words.append(w1_part)
-        load_x(2)
-        load_x(3)
+            w1_raw.append(w1_part)
         load_scales(w2_scales, W2_scales)
         w2_words = consts.tile([P, PASSES, OUT], U32, align_bytes=64)
         nc.sync.dma_start(
             out=w2_words[:].bitcast(I32),
             in_=W2_words.rearrange("g p n t -> p g (n t)").bitcast(I32),
         )
-        for i in range(4, ROW_TILES):
-            load_x(i)
         b2_spread = consts.tile([P, OUT], BF16)
         nc.sync.dma_start(out=b2_spread[:], in_=b2.partition_broadcast(P))
 
-        b1_sorted = consts.tile([P, HIDDEN_BANKS, 2, P, 2], F32)
+        w1_codes = consts.tile([P, PASSES, PACK, PASSES, P], I32, align_bytes=64)
+        w1_plane = consts.tile([P, PASSES, PACK, PASSES, P], U8, align_bytes=64)
 
-        def spread_b1():
-            for j in range(HIDDEN_BANKS):
-                spread = psum.tile([P, BANK], F32, tag="h_acc", bufs=4)
-                nc.tensor.matmul(
-                    out=spread[:],
-                    lhsT=ones[:],
-                    rhs=bias_rows[:, j * BANK : (j + 1) * BANK],
-                    start=True,
-                    stop=True,
-                )
-                nc.scalar.copy(
-                    out=b1_sorted[:, j],
-                    in_=spread[:].rearrange("r (p u e) -> r u p e", u=2, e=2),
-                )
+        def sort_w1_scales(t):
+            nc.vector.tensor_copy(
+                out=w1_plane[:, :, t, :, :].rearrange("p c g m -> p g c m"),
+                in_=w1_scales_raw[:, t : PASSES * HIDDEN : PACK].rearrange(
+                    "p (g c m) -> p g c m", g=PASSES, m=P
+                ),
+            )
 
-        x_mx = {}
-        h_acc = {}
-        h_sorted = {}
-        h_grouped = {}
-        h_mx = {}
-        v_acc = {}
-        v_rows = {}
+        def sort_w1_codes(c, t):
+            nc.vector.tensor_copy(out=w1_codes[:, c, t, :, :], in_=w1_raw[c][:, :, t:K_PASS:PACK])
+
         x_grouped = {}
+        x_codes = []
+        x_plane = []
+        for b in range(BLOCKS):
+            codes = blocks.tile([P, PASSES * BLOCK], U32, align_bytes=64, tag="x_codes")
+            plane = blocks.tile([P, PASSES * BLOCK], U8, align_bytes=64, tag="x_plane")
+            x_codes.append(codes)
+            x_plane.append(plane)
 
         def transpose_x(i):
             words = x_tiles[i][:].bitcast(F32)
-            x_t = psum.tile([P, PASSES, 2, P], F32, tag="transposed", bufs=2)
+            x_t = psum.tile([P, PASSES, 2, P], F32, tag="bank")
             for g in range(PASSES):
                 for u in range(2):
                     nc.tensor.transpose(
                         x_t[:, g, u, :], words[:, 256 * g + u : 256 * (g + 1) : 2], identity[:]
                     )
-            grouped = work.tile([P, PASSES * K_PASS], BF16, align_bytes=64, tag="x_grouped")
+            grouped = x_pool.tile([P, PASSES * K_PASS], BF16, align_bytes=64, tag="x_grouped")
             nc.scalar.copy(
                 out=grouped[:].bitcast(F32).rearrange("p (g r u) -> p g r u", g=PASSES, u=2),
                 in_=x_t[:].rearrange("p g u r -> p g r u"),
             )
             x_grouped[i] = grouped
 
-        def quantise(grouped, tag):
-            codes = work.tile([P, PASSES * P], U32, align_bytes=64, tag=tag + "_codes")
-            plane = work.tile([P, PASSES * P], U8, align_bytes=64, tag=tag + "_plane")
-            nc.vector.quantize_mx(out=codes[:].bitcast(FP8X4), scales=plane[:], in_=grouped[:])
-            return codes, plane
+        def quantise_x(i):
+            b, j = divmod(i, TILES_IN_BLOCK)
+            for g in range(PASSES):
+                first = g * BLOCK + j * P
+                nc.vector.quantize_mx(
+                    out=x_codes[b][:, first : first + P].bitcast(FP8X4),
+                    scales=x_plane[b][:, first : first + P],
+                    in_=x_grouped[i][:, g * K_PASS : (g + 1) * K_PASS],
+                )
 
-        def multiply(acc, rows_mx, words, scales):
-            codes, plane = rows_mx
+        h_rows = {}
+        h_mx = {}
+
+        def multiply_w1(b, c, t):
+            if t == 0:
+                h_lin = halves.tile([P, PACK, BLOCK], BF16, tag="h_lin")
+                h_rows[(b, c)] = h_lin
+            acc = psum.tile([P, BLOCK], F32, tag="bank")
             for g in range(PASSES):
                 nc.tensor.matmul_mx(
                     out=acc[:],
-                    lhsT=codes[:, g * P : (g + 1) * P].bitcast(FP8X4),
-                    lhsT_scale=plane[:, g * P : (g + 1) * P],
-                    rhs=words[:, g, :].bitcast(FP8X4),
-                    rhs_scale=scales[:, g, :],
+                    lhsT=w1_codes[:, c, t, g, :].bitcast(FP8X4),
+                    lhsT_scale=w1_plane[:, c, t, g, :],
+                    rhs=x_codes[b][:, g * BLOCK : (g + 1) * BLOCK].bitcast(FP8X4),
+                    rhs_scale=x_plane[b][:, g * BLOCK : (g + 1) * BLOCK],
                     start=(g == 0),
                     stop=(g == PASSES - 1),
                 )
-
-        def multiply_w1(i):
-            h_acc[i] = []
-            for j in range(HIDDEN_BANKS):
-                acc = psum.tile([P, BANK], F32, tag="h_acc", bufs=4)
-                multiply(acc, x_mx[i], w1_words[j], w1_scales[:, :, j * BANK : (j + 1) * BANK])
-                h_acc[i].append(acc)
-
-        def add_b1(i):
-            biased = work.tile([P, HIDDEN_BANKS, 2, P, 2], BF16, tag="h_sorted")
-            for j in range(HIDDEN_BANKS):
-                nc.vector.tensor_tensor(
-                    out=biased[:, j],
-                    in0=h_acc[i][j][:].rearrange("r (p u e) -> r u p e", u=2, e=2),
-                    in1=b1_sorted[:, j],
-                    op=ALU.add,
-                )
-            h_sorted[i] = biased
-
-        def transpose_h(i):
-            words = h_sorted[i][:].rearrange("r g u p e -> r (g u p e)").bitcast(F32)
-            h_t = psum.tile([P, 2, PASSES, P], F32, tag="transposed", bufs=2)
-            for g in range(PASSES):
-                for u in range(2):
-                    first = (2 * g + u) * P
-                    nc.tensor.transpose(h_t[:, u, g, :], words[:, first : first + P], identity[:])
-            grouped = work.tile([P, PASSES * K_PASS], BF16, align_bytes=64, tag="h_grouped")
             nc.scalar.activation(
-                out=grouped[:].rearrange("p (c u e) -> p c u e", u=2, e=2),
-                in_=h_t[:].rearrange("p u g r -> p u (g r)").bitcast(BF16).rearrange(
-                    "p u (c e) -> p c u e", e=2
-                ),
-                func=ACT.Relu,
+                out=h_rows[(b, c)][:, t, :], in_=acc[:], func=ACT.Relu, bias=b1_cols[:, c, t : t + 1]
             )
-            h_grouped[i] = grouped
 
-        def multiply_w2(i):
-            acc = psum.tile([P, OUT], F32, tag="v_acc", bufs=2)
-            multiply(acc, h_mx[i], w2_words, w2_scales)
-            v_acc[i] = acc
+        h_grouped = {}
+
+        def interleave_h(b, c):
+            grouped = halves.tile([P, BLOCK, PACK], BF16, align_bytes=64, tag="h_grouped")
+            nc.vector.tensor_copy(out=grouped[:], in_=h_rows[(b, c)][:].rearrange("p t r -> p r t"))
+            h_grouped[(b, c)] = grouped
+
+        def quantise_h(b, c):
+            codes = halves.tile([P, BLOCK], U32, align_bytes=64, tag="h_codes")
+            plane = halves.tile([P, BLOCK], U8, align_bytes=64, tag="h_plane")
+            nc.vector.quantize_mx(
+                out=codes[:].bitcast(FP8X4),
+                scales=plane[:],
+                in_=h_grouped[(b, c)][:].rearrange("p r t -> p (r t)"),
+            )
+            h_mx[(b, c)] = (codes, plane)
+
+        v_acc = {}
+        v_rows = {}
+
+        def multiply_w2(i, passes):
+            b, j = divmod(i, TILES_IN_BLOCK)
+            if 0 in passes:
+                acc = psum.tile([P, OUT], F32, tag="bank")
+                v_acc[i] = acc
+            acc = v_acc[i]
+            for c in passes:
+                codes, plane = h_mx[(b, c)]
+                nc.tensor.matmul_mx(
+                    out=acc[:],
+                    lhsT=codes[:, j * P : (j + 1) * P].bitcast(FP8X4),
+                    lhsT_scale=plane[:, j * P : (j + 1) * P],
+                    rhs=w2_words[:, c, :].bitcast(FP8X4),
+                    rhs_scale=w2_scales[:, c, :],
+                    start=(c == 0),
+                    stop=(c == PASSES - 1),
+                )
 
         def add_b2(i):
             v = work.tile([P, OUT], F32, tag="v")
             nc.vector.tensor_tensor(out=v[:], in0=v_acc[i][:], in1=b2_spread[:], op=ALU.add)
             v_rows[i] = v
 
-        def normalise_and_store(i):
+        inverses = {}
+
+        def row_norm(i):
             v = v_rows[i]
             squares = work.tile([P, OUT], BF16, tag="squares")
             norm2 = work.tile([P, 1], F32, tag="norm2")
@@ -208,35 +217,56 @@ def tile_geometricmanifoldnetwork_pa_kernel(
             )
             inverse = work.tile([P, 1], F32, tag="inverse")
             nc.gpsimd.tensor_tensor(out=inverse[:], in0=floored[:], in1=minus_half[:], op=ALU.pow)
+            inverses[i] = inverse
+
+        def scale_and_store(i):
             unit = work.tile([P, OUT], F32, tag="unit")
-            nc.gpsimd.tensor_scalar(
-                out=unit[:], in0=v[:], scalar1=inverse[:, 0:1], scalar2=0.0, op0=ALU.mult, op1=ALU.add
-            )
+            if i < TILES_IN_BLOCK:
+                nc.scalar.activation(
+                    out=unit[:], in_=v_rows[i][:], func=ACT.Copy, scale=inverses[i][:, 0:1]
+                )
+            else:
+                nc.vector.tensor_scalar(
+                    out=unit[:], in0=v_rows[i][:], scalar1=inverses[i][:, 0:1], scalar2=None,
+                    op0=ALU.mult,
+                )
             nc.sync.dma_start(out=out[i * P : (i + 1) * P, :], in_=unit[:])
 
-        def live(i):
-            return 0 <= i < ROW_TILES
+        for t in range(PACK):
+            sort_w1_scales(t)
+        for i in range(ROW_TILES):
+            transpose_x(i)
+            quantise_x(i)
+            if i == 5:
+                for t in range(PACK):
+                    sort_w1_codes(0, t)
+        for t in range(PACK):
+            sort_w1_codes(1, t)
 
-        transpose_x(0)
-        transpose_x(1)
-        spread_b1()
-        x_mx[0] = quantise(x_grouped[0], "x")
-        for n in range(ROW_TILES + 3):
-            if live(n):
-                multiply_w1(n)
-            if live(n - 3):
-                multiply_w2(n - 3)
-            if live(n + 1):
-                x_mx[n + 1] = quantise(x_grouped[n + 1], "x")
-            if live(n):
-                add_b1(n)
-            if live(n - 2):
-                h_mx[n - 2] = quantise(h_grouped[n - 2], "h")
-            if live(n - 3):
-                add_b2(n - 3)
-            if live(n + 2):
-                transpose_x(n + 2)
-            if live(n - 1):
-                transpose_h(n - 1)
-            if live(n - 3):
-                normalise_and_store(n - 3)
+        last = (BLOCKS - 1, PASSES - 1)
+        for b in range(BLOCKS):
+            for c in range(PASSES):
+                for t in range(PACK):
+                    multiply_w1(b, c, t)
+                if (b, c) != last:
+                    interleave_h(b, c)
+                    quantise_h(b, c)
+        for i in range(TILES_IN_BLOCK):
+            multiply_w2(i, (0, 1))
+        for i in range(TILES_IN_BLOCK, ROW_TILES):
+            multiply_w2(i, (0,))
+        for i in range(TILES_IN_BLOCK):
+            add_b2(i)
+            row_norm(i)
+        interleave_h(*last)
+        quantise_h(*last)
+        for i in range(TILES_IN_BLOCK):
+            scale_and_store(i)
+        for i in range(TILES_IN_BLOCK, ROW_TILES):
+            multiply_w2(i, (1,))
+            add_b2(i)
+            row_norm(i)
+            if i - 2 >= TILES_IN_BLOCK:
+                scale_and_store(i - 2)
+        scale_and_store(ROW_TILES - 2)
+        scale_and_store(ROW_TILES - 1)

@@ -47,10 +47,12 @@ def tile_geometricmanifoldnetwork_pa_kernel(
         w2_scales = consts.tile([P, PASSES, OUT], U8, align_bytes=64)
         nc.vector.memset(w1_scales_raw[:].bitcast(I32), 0)
         nc.vector.memset(w2_scales[:].bitcast(I32), 0)
-        minus_half = consts.tile([P, 1], F32)
-        nc.vector.memset(minus_half[:], -0.5)
+        floor2 = consts.tile([P, 1], F32)
+        nc.vector.memset(floor2[:], EPS * EPS)
+        minus_floor2 = consts.tile([P, 1], F32)
+        nc.vector.memset(minus_floor2[:], -EPS * EPS)
         warm = consts.tile([P, 1], F32)
-        nc.scalar.activation(out=warm[:], in_=minus_half[:], func=ACT.Relu)
+        nc.scalar.activation(out=warm[:], in_=floor2[:], func=ACT.Abs_reciprocal_sqrt)
         identity = consts.tile([P, P], F32)
         masks.make_identity(nc, identity[:])
 
@@ -211,12 +213,12 @@ def tile_geometricmanifoldnetwork_pa_kernel(
             squares = work.tile([P, OUT], BF16, tag="squares")
             norm2 = work.tile([P, 1], F32, tag="norm2")
             nc.scalar.activation(out=squares[:], in_=v[:], func=ACT.Square, accum_out=norm2[:])
-            floored = work.tile([P, 1], F32, tag="floored")
-            nc.gpsimd.tensor_scalar(
-                out=floored[:], in0=norm2[:], scalar1=EPS * EPS, scalar2=None, op0=ALU.max
-            )
+            above = work.tile([P, 1], F32, tag="above")
+            nc.scalar.activation(out=above[:], in_=norm2[:], func=ACT.Relu, bias=minus_floor2[:, 0:1])
             inverse = work.tile([P, 1], F32, tag="inverse")
-            nc.gpsimd.tensor_tensor(out=inverse[:], in0=floored[:], in1=minus_half[:], op=ALU.pow)
+            nc.scalar.activation(
+                out=inverse[:], in_=above[:], func=ACT.Abs_reciprocal_sqrt, bias=floor2[:, 0:1]
+            )
             inverses[i] = inverse
 
         def scale_and_store(i):

@@ -93,7 +93,7 @@ def tile_geometricmanifoldnetwork_pa_kernel(
         b2_spread = consts.tile([P, OUT], BF16)
         nc.sync.dma_start(out=b2_spread[:], in_=b2.partition_broadcast(P))
 
-        w1_codes = consts.tile([P, PASSES, PACK, PASSES, P], I32, align_bytes=64)
+        w1_codes = consts.tile([P, PASSES, PASSES, PACK, P], I32, align_bytes=64)
         w1_plane = consts.tile([P, PASSES, PACK, PASSES, P], U8, align_bytes=64)
 
         def sort_w1_scales(t):
@@ -104,8 +104,11 @@ def tile_geometricmanifoldnetwork_pa_kernel(
                 ),
             )
 
-        def sort_w1_codes(c, t):
-            nc.vector.tensor_copy(out=w1_codes[:, c, t, :, :], in_=w1_raw[c][:, :, t:K_PASS:PACK])
+        def sort_w1_codes(c, g):
+            nc.vector.tensor_copy(
+                out=w1_codes[:, c, g, :, :].rearrange("p t m -> p m t"),
+                in_=w1_raw[c][:, g, :].rearrange("p (m t) -> p m t", t=PACK),
+            )
 
         x_grouped = {}
         x_codes = []
@@ -116,30 +119,31 @@ def tile_geometricmanifoldnetwork_pa_kernel(
             x_codes.append(codes)
             x_plane.append(plane)
 
-        def transpose_x(i):
-            words = x_tiles[i][:].bitcast(F32)
-            x_t = psum.tile([P, PASSES, 2, P], F32, tag="bank")
-            for g in range(PASSES):
+        def transpose_x(pair, g):
+            b, half = divmod(pair, TILES_IN_BLOCK // 2)
+            x_t = psum.tile([P, 2, 2, P], F32, tag="bank")
+            for e in range(2):
+                words = x_tiles[2 * pair + e][:].bitcast(F32)
                 for u in range(2):
                     nc.tensor.transpose(
-                        x_t[:, g, u, :], words[:, 256 * g + u : 256 * (g + 1) : 2], identity[:]
+                        x_t[:, e, u, :], words[:, 256 * g + u : 256 * (g + 1) : 2], identity[:]
                     )
-            grouped = x_pool.tile([P, PASSES * K_PASS], BF16, align_bytes=64, tag="x_grouped")
+            if half == 0:
+                grouped = halves.tile([P, BLOCK * PACK], BF16, align_bytes=64, tag="x_grouped")
+                x_grouped[(b, g)] = grouped
             nc.scalar.copy(
-                out=grouped[:].bitcast(F32).rearrange("p (g r u) -> p g r u", g=PASSES, u=2),
-                in_=x_t[:].rearrange("p g u r -> p g r u"),
+                out=x_grouped[(b, g)][:, half * 2 * K_PASS : (half + 1) * 2 * K_PASS]
+                .bitcast(F32)
+                .rearrange("p (e r u) -> p e r u", e=2, u=2),
+                in_=x_t[:].rearrange("p e u r -> p e r u"),
             )
-            x_grouped[i] = grouped
 
-        def quantise_x(i):
-            b, j = divmod(i, TILES_IN_BLOCK)
-            for g in range(PASSES):
-                first = g * BLOCK + j * P
-                nc.vector.quantize_mx(
-                    out=x_codes[b][:, first : first + P].bitcast(FP8X4),
-                    scales=x_plane[b][:, first : first + P],
-                    in_=x_grouped[i][:, g * K_PASS : (g + 1) * K_PASS],
-                )
+        def quantise_x(b, g):
+            nc.vector.quantize_mx(
+                out=x_codes[b][:, g * BLOCK : (g + 1) * BLOCK].bitcast(FP8X4),
+                scales=x_plane[b][:, g * BLOCK : (g + 1) * BLOCK],
+                in_=x_grouped[(b, g)][:],
+            )
 
         h_rows = {}
         h_mx = {}
@@ -152,7 +156,7 @@ def tile_geometricmanifoldnetwork_pa_kernel(
             for g in range(PASSES):
                 nc.tensor.matmul_mx(
                     out=acc[:],
-                    lhsT=w1_codes[:, c, t, g, :].bitcast(FP8X4),
+                    lhsT=w1_codes[:, c, g, t, :].bitcast(FP8X4),
                     lhsT_scale=w1_plane[:, c, t, g, :],
                     rhs=x_codes[b][:, g * BLOCK : (g + 1) * BLOCK].bitcast(FP8X4),
                     rhs_scale=x_plane[b][:, g * BLOCK : (g + 1) * BLOCK],
@@ -236,14 +240,18 @@ def tile_geometricmanifoldnetwork_pa_kernel(
 
         for t in range(PACK):
             sort_w1_scales(t)
-        for i in range(ROW_TILES):
-            transpose_x(i)
-            quantise_x(i)
-            if i == 5:
-                for t in range(PACK):
-                    sort_w1_codes(0, t)
-        for t in range(PACK):
-            sort_w1_codes(1, t)
+        for b in range(BLOCKS):
+            for pair in range(2 * b, 2 * b + 2):
+                for g in range(PASSES):
+                    transpose_x(pair, g)
+            if b == 0:
+                for g in range(PASSES):
+                    quantise_x(b, g)
+        for c in range(PASSES):
+            for g in range(PASSES):
+                sort_w1_codes(c, g)
+        for g in range(PASSES):
+            quantise_x(1, g)
 
         last = (BLOCKS - 1, PASSES - 1)
         for b in range(BLOCKS):

@@ -36,7 +36,7 @@ def tile_geometricmanifoldnetwork_pa_kernel(
     nc = tc.nc
     with ExitStack() as ctx:
         consts = ctx.enter_context(tc.tile_pool(name="consts", bufs=1))
-        x_pool = ctx.enter_context(tc.tile_pool(name="x_pool", bufs=ROW_TILES))
+        x_pool = ctx.enter_context(tc.tile_pool(name="x_pool", bufs=ROW_TILES // 2))
         blocks = ctx.enter_context(tc.tile_pool(name="blocks", bufs=BLOCKS))
         halves = ctx.enter_context(tc.tile_pool(name="halves", bufs=BLOCKS * PASSES))
         work = ctx.enter_context(tc.tile_pool(name="work", bufs=ROW_TILES))
@@ -68,12 +68,15 @@ def tile_geometricmanifoldnetwork_pa_kernel(
                     in_=scales[:, 4 * q : 4 * q + 4, :].bitcast(I32).rearrange("g r n -> r g n"),
                 )
 
-        x_tiles = []
-        for i in range(ROW_TILES):
-            x_tile = x_pool.tile([P, PASSES * K_PASS], BF16)
-            nc.sync.dma_start(out=x_tile[:], in_=x[i * P : (i + 1) * P, :])
-            x_tiles.append(x_tile)
-            if i == 0:
+        x_pairs = []
+        for pair in range(ROW_TILES // 2):
+            x_pair = x_pool.tile([P, 2, PASSES * K_PASS], BF16)
+            nc.sync.dma_start(
+                out=x_pair[:],
+                in_=x[2 * pair * P : 2 * (pair + 1) * P, :].rearrange("(e p) k -> p e k", e=2),
+            )
+            x_pairs.append(x_pair)
+            if pair == 0:
                 load_scales(w1_scales_raw[:].rearrange("p (g n) -> p g n", g=PASSES), W1_scales)
         w1_bytes = W1_words.rearrange("g p n t -> p g (n t)")
         w1_raw = []
@@ -123,7 +126,7 @@ def tile_geometricmanifoldnetwork_pa_kernel(
             b, half = divmod(pair, TILES_IN_BLOCK // 2)
             x_t = psum.tile([P, 2, 2, P], F32, tag="bank")
             for e in range(2):
-                words = x_tiles[2 * pair + e][:].bitcast(F32)
+                words = x_pairs[pair][:, e, :].bitcast(F32)
                 for u in range(2):
                     nc.tensor.transpose(
                         x_t[:, e, u, :], words[:, 256 * g + u : 256 * (g + 1) : 2], identity[:]
@@ -212,29 +215,42 @@ def tile_geometricmanifoldnetwork_pa_kernel(
 
         inverses = {}
 
-        def row_norm(i):
-            v = v_rows[i]
-            squares = work.tile([P, OUT], BF16, tag="squares")
-            norm2 = work.tile([P, 1], F32, tag="norm2")
-            nc.scalar.activation(out=squares[:], in_=v[:], func=ACT.Square, accum_out=norm2[:])
-            above = work.tile([P, 1], F32, tag="above")
-            nc.scalar.activation(out=above[:], in_=norm2[:], func=ACT.Relu, bias=minus_floor2[:, 0:1])
-            inverse = work.tile([P, 1], F32, tag="inverse")
-            nc.scalar.activation(
-                out=inverse[:], in_=above[:], func=ACT.Abs_reciprocal_sqrt, bias=floor2[:, 0:1]
-            )
-            inverses[i] = inverse
+        norms = {}
 
-        def scale_and_store(i):
-            unit = work.tile([P, OUT], F32, tag="unit")
-            if i < TILES_IN_BLOCK:
+        def row_norm(i):
+            pair, e = divmod(i, 2)
+            if e == 0:
+                norm2 = work.tile([P, 2], F32, tag="norm2")
+                norms[pair] = norm2
+            squares = work.tile([P, OUT], BF16, tag="squares")
+            nc.scalar.activation(
+                out=squares[:], in_=v_rows[i][:], func=ACT.Square, accum_out=norms[pair][:, e : e + 1]
+            )
+            if e == 1:
+                above = work.tile([P, 2], F32, tag="above")
                 nc.scalar.activation(
-                    out=unit[:], in_=v_rows[i][:], func=ACT.Copy, scale=inverses[i][:, 0:1]
+                    out=above[:], in_=norms[pair][:], func=ACT.Relu, bias=minus_floor2[:, 0:1]
+                )
+                inverse = work.tile([P, 2], F32, tag="inverse")
+                nc.scalar.activation(
+                    out=inverse[:], in_=above[:], func=ACT.Abs_reciprocal_sqrt, bias=floor2[:, 0:1]
+                )
+                inverses[pair] = inverse
+
+        def scale_and_store(i, engine):
+            pair, e = divmod(i, 2)
+            factor = inverses[pair][:, e : e + 1]
+            unit = work.tile([P, OUT], F32, tag="unit")
+            if engine == "scalar":
+                nc.scalar.activation(out=unit[:], in_=v_rows[i][:], func=ACT.Copy, scale=factor)
+            elif engine == "vector":
+                nc.vector.tensor_scalar(
+                    out=unit[:], in0=v_rows[i][:], scalar1=factor, scalar2=None, op0=ALU.mult
                 )
             else:
-                nc.vector.tensor_scalar(
-                    out=unit[:], in0=v_rows[i][:], scalar1=inverses[i][:, 0:1], scalar2=None,
-                    op0=ALU.mult,
+                nc.gpsimd.tensor_scalar(
+                    out=unit[:], in0=v_rows[i][:], scalar1=factor, scalar2=0.0, op0=ALU.mult,
+                    op1=ALU.add,
                 )
             nc.sync.dma_start(out=out[i * P : (i + 1) * P, :], in_=unit[:])
 
@@ -253,30 +269,38 @@ def tile_geometricmanifoldnetwork_pa_kernel(
         for g in range(PASSES):
             quantise_x(1, g)
 
-        last = (BLOCKS - 1, PASSES - 1)
         for b in range(BLOCKS):
             for c in range(PASSES):
                 for t in range(PACK):
                     multiply_w1(b, c, t)
-                if (b, c) != last:
+                if b == 0:
                     interleave_h(b, c)
                     quantise_h(b, c)
         for i in range(TILES_IN_BLOCK):
             multiply_w2(i, (0, 1))
+        interleave_h(1, 0)
+        add_b2(0)
+        row_norm(0)
+        quantise_h(1, 0)
         for i in range(TILES_IN_BLOCK, ROW_TILES):
             multiply_w2(i, (0,))
-        for i in range(TILES_IN_BLOCK):
-            add_b2(i)
-            row_norm(i)
-        interleave_h(*last)
-        quantise_h(*last)
-        for i in range(TILES_IN_BLOCK):
-            scale_and_store(i)
+        add_b2(1)
+        row_norm(1)
+        add_b2(2)
+        row_norm(2)
+        interleave_h(1, 1)
+        add_b2(3)
+        row_norm(3)
+        quantise_h(1, 1)
+        scale_and_store(0, "scalar")
+        scale_and_store(1, "scalar")
+        scale_and_store(2, "gpsimd")
+        scale_and_store(3, "gpsimd")
         for i in range(TILES_IN_BLOCK, ROW_TILES):
             multiply_w2(i, (1,))
             add_b2(i)
             row_norm(i)
-            if i - 2 >= TILES_IN_BLOCK:
-                scale_and_store(i - 2)
-        scale_and_store(ROW_TILES - 2)
-        scale_and_store(ROW_TILES - 1)
+        scale_and_store(4, "gpsimd")
+        scale_and_store(5, "gpsimd")
+        scale_and_store(6, "gpsimd")
+        scale_and_store(7, "vector")

@@ -166,15 +166,30 @@ def tile_geometricmanifoldnetwork_pa_kernel(
                     start=(g == 0),
                     stop=(g == PASSES - 1),
                 )
-            nc.scalar.activation(
-                out=h_rows[(b, c)][:, t, :], in_=acc[:], func=ACT.Relu, bias=b1_cols[:, c, t : t + 1]
-            )
+            if (b, c) == (1, 1) and t % 2 == 1:
+                nc.vector.tensor_scalar(
+                    out=h_rows[(b, c)][:, t, :], in0=acc[:], scalar1=b1_cols[:, c, t : t + 1],
+                    scalar2=0.0, op0=ALU.add, op1=ALU.max,
+                )
+            else:
+                nc.scalar.activation(
+                    out=h_rows[(b, c)][:, t, :], in_=acc[:], func=ACT.Relu,
+                    bias=b1_cols[:, c, t : t + 1],
+                )
 
         h_grouped = {}
 
-        def interleave_h(b, c):
+        def interleave_h(b, c, on_gpsimd=False):
             grouped = halves.tile([P, BLOCK, PACK], BF16, align_bytes=64, tag="h_grouped")
-            nc.vector.tensor_copy(out=grouped[:], in_=h_rows[(b, c)][:].rearrange("p t r -> p r t"))
+            if on_gpsimd:
+                nc.gpsimd.tensor_scalar(
+                    out=grouped[:], in0=h_rows[(b, c)][:].rearrange("p t r -> p r t"), scalar1=1.0,
+                    scalar2=0.0, op0=ALU.mult, op1=ALU.add,
+                )
+            else:
+                nc.vector.tensor_copy(
+                    out=grouped[:], in_=h_rows[(b, c)][:].rearrange("p t r -> p r t")
+                )
             h_grouped[(b, c)] = grouped
 
         def quantise_h(b, c):
@@ -278,22 +293,22 @@ def tile_geometricmanifoldnetwork_pa_kernel(
                     quantise_h(b, c)
         for i in range(TILES_IN_BLOCK):
             multiply_w2(i, (0, 1))
-        interleave_h(1, 0)
+        interleave_h(1, 0, on_gpsimd=True)
         add_b2(0)
         row_norm(0)
+        add_b2(1)
+        row_norm(1)
         quantise_h(1, 0)
         for i in range(TILES_IN_BLOCK, ROW_TILES):
             multiply_w2(i, (0,))
-        add_b2(1)
-        row_norm(1)
+        interleave_h(1, 1)
         add_b2(2)
         row_norm(2)
-        interleave_h(1, 1)
+        quantise_h(1, 1)
         add_b2(3)
         row_norm(3)
-        quantise_h(1, 1)
-        scale_and_store(0, "scalar")
-        scale_and_store(1, "scalar")
+        scale_and_store(0, "gpsimd")
+        scale_and_store(1, "gpsimd")
         scale_and_store(2, "gpsimd")
         scale_and_store(3, "gpsimd")
         for i in range(TILES_IN_BLOCK, ROW_TILES):
@@ -302,5 +317,5 @@ def tile_geometricmanifoldnetwork_pa_kernel(
             row_norm(i)
         scale_and_store(4, "gpsimd")
         scale_and_store(5, "gpsimd")
-        scale_and_store(6, "gpsimd")
+        scale_and_store(6, "scalar")
         scale_and_store(7, "vector")

@@ -166,41 +166,34 @@ def tile_geometricmanifoldnetwork_pa_kernel(
                     start=(g == 0),
                     stop=(g == PASSES - 1),
                 )
-            if (b, c) == (1, 1) and t % 2 == 1:
-                nc.vector.tensor_scalar(
-                    out=h_rows[(b, c)][:, t, :], in0=acc[:], scalar1=b1_cols[:, c, t : t + 1],
-                    scalar2=0.0, op0=ALU.add, op1=ALU.max,
-                )
-            else:
-                nc.scalar.activation(
-                    out=h_rows[(b, c)][:, t, :], in_=acc[:], func=ACT.Relu,
-                    bias=b1_cols[:, c, t : t + 1],
-                )
+            nc.scalar.activation(
+                out=h_rows[(b, c)][:, t, :], in_=acc[:], func=ACT.Relu, bias=b1_cols[:, c, t : t + 1]
+            )
 
         h_grouped = {}
 
-        def interleave_h(b, c, on_gpsimd=False):
-            grouped = halves.tile([P, BLOCK, PACK], BF16, align_bytes=64, tag="h_grouped")
+        def interleave_h(b, c, first=0, rows=BLOCK, on_gpsimd=False):
+            grouped = halves.tile([P, rows, PACK], BF16, align_bytes=64, name="h_grouped_%d%d%d" % (b, c, first), bufs=1)
+            planes = h_rows[(b, c)][:, :, first : first + rows].rearrange("p t r -> p r t")
             if on_gpsimd:
                 nc.gpsimd.tensor_scalar(
-                    out=grouped[:], in0=h_rows[(b, c)][:].rearrange("p t r -> p r t"), scalar1=1.0,
-                    scalar2=0.0, op0=ALU.mult, op1=ALU.add,
+                    out=grouped[:], in0=planes, scalar1=1.0, scalar2=0.0, op0=ALU.mult, op1=ALU.add
                 )
             else:
-                nc.vector.tensor_copy(
-                    out=grouped[:], in_=h_rows[(b, c)][:].rearrange("p t r -> p r t")
-                )
-            h_grouped[(b, c)] = grouped
+                nc.vector.tensor_copy(out=grouped[:], in_=planes)
+            h_grouped[(b, c, first)] = grouped
 
-        def quantise_h(b, c):
-            codes = halves.tile([P, BLOCK], U32, align_bytes=64, tag="h_codes")
-            plane = halves.tile([P, BLOCK], U8, align_bytes=64, tag="h_plane")
+        def quantise_h(b, c, first=0, rows=BLOCK):
+            if first == 0:
+                codes = halves.tile([P, BLOCK], U32, align_bytes=64, tag="h_codes")
+                plane = halves.tile([P, BLOCK], U8, align_bytes=64, tag="h_plane")
+                h_mx[(b, c)] = (codes, plane)
+            codes, plane = h_mx[(b, c)]
             nc.vector.quantize_mx(
-                out=codes[:].bitcast(FP8X4),
-                scales=plane[:],
-                in_=h_grouped[(b, c)][:].rearrange("p r t -> p (r t)"),
+                out=codes[:, first : first + rows].bitcast(FP8X4),
+                scales=plane[:, first : first + rows],
+                in_=h_grouped[(b, c, first)][:].rearrange("p r t -> p (r t)"),
             )
-            h_mx[(b, c)] = (codes, plane)
 
         v_acc = {}
         v_rows = {}
@@ -284,38 +277,44 @@ def tile_geometricmanifoldnetwork_pa_kernel(
         for g in range(PASSES):
             quantise_x(1, g)
 
-        for b in range(BLOCKS):
-            for c in range(PASSES):
-                for t in range(PACK):
-                    multiply_w1(b, c, t)
-                if b == 0:
-                    interleave_h(b, c)
-                    quantise_h(b, c)
+        half = BLOCK // 2
+        for c in range(PASSES):
+            for t in range(PACK):
+                multiply_w1(0, c, t)
+            interleave_h(0, c)
+            quantise_h(0, c)
+        for t in range(PACK):
+            multiply_w1(1, 0, t)
+        interleave_h(1, 0)
+        for t in range(PACK):
+            multiply_w1(1, 1, t)
+        quantise_h(1, 0)
         for i in range(TILES_IN_BLOCK):
             multiply_w2(i, (0, 1))
-        interleave_h(1, 0, on_gpsimd=True)
-        add_b2(0)
-        row_norm(0)
-        add_b2(1)
-        row_norm(1)
-        quantise_h(1, 0)
         for i in range(TILES_IN_BLOCK, ROW_TILES):
             multiply_w2(i, (0,))
-        interleave_h(1, 1)
-        add_b2(2)
-        row_norm(2)
-        quantise_h(1, 1)
-        add_b2(3)
-        row_norm(3)
+        add_b2(0)
+        row_norm(0)
+        interleave_h(1, 1, 0, half)
+        interleave_h(1, 1, half, half, on_gpsimd=True)
+        add_b2(1)
+        row_norm(1)
         scale_and_store(0, "gpsimd")
         scale_and_store(1, "gpsimd")
+        quantise_h(1, 1, 0, half)
+        add_b2(2)
+        row_norm(2)
+        quantise_h(1, 1, half, half)
+        add_b2(3)
+        row_norm(3)
         scale_and_store(2, "gpsimd")
         scale_and_store(3, "gpsimd")
         for i in range(TILES_IN_BLOCK, ROW_TILES):
             multiply_w2(i, (1,))
             add_b2(i)
             row_norm(i)
-        scale_and_store(4, "gpsimd")
-        scale_and_store(5, "gpsimd")
-        scale_and_store(6, "scalar")
+            if i == 5:
+                scale_and_store(4, "gpsimd")
+                scale_and_store(5, "gpsimd")
+        scale_and_store(6, "vector")
         scale_and_store(7, "vector")

@@ -43,8 +43,8 @@ def tile_geometricmanifoldnetwork_pa_kernel(
         psum = ctx.enter_context(tc.psum_pool(name="psum", bufs=8))
         ctx.enter_context(tc.manual_schedule())
 
-        w1_scales_raw = consts.tile([P, PASSES * HIDDEN], U8, align_bytes=64)
-        w2_scales = consts.tile([P, PASSES, OUT], U8, align_bytes=64)
+        w1_scales_raw = consts.tile([P, HIDDEN], U8, align_bytes=64)
+        w2_scales = consts.tile([P, OUT], U8, align_bytes=64)
         nc.vector.memset(w1_scales_raw[:].bitcast(I32), 0)
         nc.vector.memset(w2_scales[:].bitcast(I32), 0)
         floor2 = consts.tile([P, 1], F32)
@@ -56,16 +56,11 @@ def tile_geometricmanifoldnetwork_pa_kernel(
         identity = consts.tile([P, P], F32)
         masks.make_identity(nc, identity[:])
 
-        b1_bf = consts.tile([P, PASSES, PACK], BF16)
-        nc.scalar.dma_start(out=b1_bf[:], in_=b1.rearrange("(c p t) -> p c t", c=PASSES, t=PACK))
-        b1_cols = consts.tile([P, PASSES, PACK], F32)
-        nc.gpsimd.tensor_copy(out=b1_cols[:], in_=b1_bf[:])
-
         def load_scales(plane, scales):
             for q in range(QUADRANTS):
                 nc.sync.dma_start(
-                    out=plane[32 * q : 32 * q + 4].bitcast(I32),
-                    in_=scales[:, 4 * q : 4 * q + 4, :].bitcast(I32).rearrange("g r n -> r g n"),
+                    out=plane[32 * q : 32 * q + 4 * PASSES, :].bitcast(I32),
+                    in_=scales[:, 4 * q : 4 * q + 4, :].bitcast(I32),
                 )
 
         x_pairs = []
@@ -77,7 +72,7 @@ def tile_geometricmanifoldnetwork_pa_kernel(
             )
             x_pairs.append(x_pair)
             if pair == 0:
-                load_scales(w1_scales_raw[:].rearrange("p (g n) -> p g n", g=PASSES), W1_scales)
+                load_scales(w1_scales_raw, W1_scales)
         w1_bytes = W1_words.rearrange("g p n t -> p g (n t)")
         w1_raw = []
         for c in range(PASSES):
@@ -87,6 +82,13 @@ def tile_geometricmanifoldnetwork_pa_kernel(
                 in_=w1_bytes[:, :, 4 * K_PASS * c : 4 * K_PASS * (c + 1)].bitcast(I32),
             )
             w1_raw.append(w1_part)
+            if c == 0:
+                b1_bf = consts.tile([P, PASSES, PACK], BF16)
+                nc.sync.dma_start(
+                    out=b1_bf[:], in_=b1.rearrange("(c p t) -> p c t", c=PASSES, t=PACK)
+                )
+                b1_cols = consts.tile([P, PASSES, PACK], F32)
+                nc.gpsimd.tensor_copy(out=b1_cols[:], in_=b1_bf[:])
         load_scales(w2_scales, W2_scales)
         w2_words = consts.tile([P, PASSES, OUT], U32, align_bytes=64)
         nc.sync.dma_start(
@@ -97,13 +99,13 @@ def tile_geometricmanifoldnetwork_pa_kernel(
         nc.sync.dma_start(out=b2_spread[:], in_=b2.partition_broadcast(P))
 
         w1_codes = consts.tile([P, PASSES, PASSES, PACK, P], I32, align_bytes=64)
-        w1_plane = consts.tile([P, PASSES, PACK, PASSES, P], U8, align_bytes=64)
+        w1_plane = consts.tile([P, PASSES, PACK, P], U8, align_bytes=64)
 
-        def sort_w1_scales(t):
+        def sort_w1_scales(c):
             nc.vector.tensor_copy(
-                out=w1_plane[:, :, t, :, :].rearrange("p c g m -> p g c m"),
-                in_=w1_scales_raw[:, t : PASSES * HIDDEN : PACK].rearrange(
-                    "p (g c m) -> p g c m", g=PASSES, m=P
+                out=w1_plane[:, c, :, :],
+                in_=w1_scales_raw[:, c * K_PASS : (c + 1) * K_PASS].rearrange(
+                    "p (m t) -> p t m", t=PACK
                 ),
             )
 
@@ -160,7 +162,7 @@ def tile_geometricmanifoldnetwork_pa_kernel(
                 nc.tensor.matmul_mx(
                     out=acc[:],
                     lhsT=w1_codes[:, c, g, t, :].bitcast(FP8X4),
-                    lhsT_scale=w1_plane[:, c, t, g, :],
+                    lhsT_scale=w1_plane[4 * g : P, c, t, :],
                     rhs=x_codes[b][:, g * BLOCK : (g + 1) * BLOCK].bitcast(FP8X4),
                     rhs_scale=x_plane[b][:, g * BLOCK : (g + 1) * BLOCK],
                     start=(g == 0),
@@ -211,7 +213,7 @@ def tile_geometricmanifoldnetwork_pa_kernel(
                     lhsT=codes[:, j * P : (j + 1) * P].bitcast(FP8X4),
                     lhsT_scale=plane[:, j * P : (j + 1) * P],
                     rhs=w2_words[:, c, :].bitcast(FP8X4),
-                    rhs_scale=w2_scales[:, c, :],
+                    rhs_scale=w2_scales[4 * c : P, :],
                     start=(c == 0),
                     stop=(c == PASSES - 1),
                 )
@@ -262,8 +264,6 @@ def tile_geometricmanifoldnetwork_pa_kernel(
                 )
             nc.sync.dma_start(out=out[i * P : (i + 1) * P, :], in_=unit[:])
 
-        for t in range(PACK):
-            sort_w1_scales(t)
         for b in range(BLOCKS):
             for pair in range(2 * b, 2 * b + 2):
                 for g in range(PASSES):
@@ -271,7 +271,11 @@ def tile_geometricmanifoldnetwork_pa_kernel(
             if b == 0:
                 for g in range(PASSES):
                     quantise_x(b, g)
+                    if g == 0:
+                        sort_w1_scales(0)
         for c in range(PASSES):
+            if c == 1:
+                sort_w1_scales(1)
             for g in range(PASSES):
                 sort_w1_codes(c, g)
         for g in range(PASSES):

@@ -45,6 +45,8 @@ def tile_geometricmanifoldnetwork_pa_kernel(
 
         w1_scales_raw = consts.tile([P, HIDDEN], U8, align_bytes=64)
         w2_scales = consts.tile([P, OUT], U8, align_bytes=64)
+        zeros = consts.tile([P, BANK], BF16)
+        nc.vector.memset(zeros[:], 0.0)
         nc.vector.memset(w1_scales_raw[:].bitcast(I32), 0)
         nc.vector.memset(w2_scales[:].bitcast(I32), 0)
         floor2 = consts.tile([P, 1], F32)
@@ -124,9 +126,15 @@ def tile_geometricmanifoldnetwork_pa_kernel(
             x_codes.append(codes)
             x_plane.append(plane)
 
+        def warm_up(bank):
+            nc.tensor.matmul(bank, lhsT=zeros[:, 0:P], rhs=zeros[:], start=True, stop=True)
+
         def transpose_x(pair, g):
             b, half = divmod(pair, TILES_IN_BLOCK // 2)
             x_t = psum.tile([P, 2, 2, P], F32, tag="bank")
+            if g == 0:
+                for n in range((6, 0, 1, 0)[pair]):
+                    warm_up(x_t[:].rearrange("p e u r -> p (e u r)"))
             for e in range(2):
                 words = x_pairs[pair][:, e, :].bitcast(F32)
                 for u in range(2):
@@ -158,6 +166,9 @@ def tile_geometricmanifoldnetwork_pa_kernel(
                 h_lin = halves.tile([P, PACK, BLOCK], BF16, tag="h_lin")
                 h_rows[(b, c)] = h_lin
             acc = psum.tile([P, BLOCK], F32, tag="bank")
+            if (b, c, t) == (0, 0, 0):
+                for n in range(2):
+                    warm_up(acc[:])
             for g in range(PASSES):
                 nc.tensor.matmul_mx(
                     out=acc[:],

@@ -185,16 +185,18 @@ def tile_geometricmanifoldnetwork_pa_kernel(
 
         h_grouped = {}
 
-        def interleave_h(b, c, first=0, rows=BLOCK, on_gpsimd=False):
+        def group_tile(b, c, first=0, rows=BLOCK):
             grouped = halves.tile([P, rows, PACK], BF16, align_bytes=64, name="h_grouped_%d%d%d" % (b, c, first), bufs=1)
-            planes = h_rows[(b, c)][:, :, first : first + rows].rearrange("p t r -> p r t")
-            if on_gpsimd:
-                nc.gpsimd.tensor_scalar(
-                    out=grouped[:], in0=planes, scalar1=1.0, scalar2=0.0, op0=ALU.mult, op1=ALU.add
-                )
-            else:
-                nc.vector.tensor_copy(out=grouped[:], in_=planes)
             h_grouped[(b, c, first)] = grouped
+
+        def interleave_h(b, c, tile_first=0, first=0, rows=BLOCK, on_scalar=False):
+            at = first - tile_first
+            dst = h_grouped[(b, c, tile_first)][:, at : at + rows, :]
+            planes = h_rows[(b, c)][:, :, first : first + rows].rearrange("p t r -> p r t")
+            if on_scalar:
+                nc.scalar.copy(out=dst, in_=planes)
+            else:
+                nc.vector.tensor_copy(out=dst, in_=planes)
 
         def quantise_h(b, c, first=0, rows=BLOCK):
             if first == 0:
@@ -296,10 +298,12 @@ def tile_geometricmanifoldnetwork_pa_kernel(
         for c in range(PASSES):
             for t in range(PACK):
                 multiply_w1(0, c, t)
+            group_tile(0, c)
             interleave_h(0, c)
             quantise_h(0, c)
         for t in range(PACK):
             multiply_w1(1, 0, t)
+        group_tile(1, 0)
         interleave_h(1, 0)
         for t in range(PACK):
             multiply_w1(1, 1, t)
@@ -308,10 +312,13 @@ def tile_geometricmanifoldnetwork_pa_kernel(
             multiply_w2(i, (0, 1))
         for i in range(TILES_IN_BLOCK, ROW_TILES):
             multiply_w2(i, (0,))
+        group_tile(1, 1, 0, half)
+        group_tile(1, 1, half, half)
+        interleave_h(1, 1, half, half + P, P, on_scalar=True)
         add_b2(0)
         row_norm(0)
-        interleave_h(1, 1, 0, half)
-        interleave_h(1, 1, half, half, on_gpsimd=True)
+        interleave_h(1, 1, 0, 0, half)
+        interleave_h(1, 1, half, half, P)
         add_b2(1)
         row_norm(1)
         scale_and_store(0, "gpsimd")

@@ -45,7 +45,7 @@ def tile_geometricmanifoldnetwork_pa_kernel(
 
         w1_scales_raw = consts.tile([P, HIDDEN], U8, align_bytes=64)
         w2_scales = consts.tile([P, OUT], U8, align_bytes=64)
-        zeros = consts.tile([P, BANK], BF16)
+        zeros = consts.tile([P, P], BF16)
         nc.vector.memset(zeros[:], 0.0)
         nc.vector.memset(w1_scales_raw[:].bitcast(I32), 0)
         nc.vector.memset(w2_scales[:].bitcast(I32), 0)
@@ -127,14 +127,14 @@ def tile_geometricmanifoldnetwork_pa_kernel(
             x_plane.append(plane)
 
         def warm_up(bank):
-            nc.tensor.matmul(bank, lhsT=zeros[:, 0:P], rhs=zeros[:], start=True, stop=True)
+            nc.tensor.matmul(bank, lhsT=zeros[:], rhs=zeros[:], start=True, stop=True)
 
         def transpose_x(pair, g):
             b, half = divmod(pair, TILES_IN_BLOCK // 2)
             x_t = psum.tile([P, 2, 2, P], F32, tag="bank")
             if g == 0:
-                for n in range((6, 0, 1, 0)[pair]):
-                    warm_up(x_t[:].rearrange("p e u r -> p (e u r)"))
+                for n in range((18, 0, 4, 0)[pair]):
+                    warm_up(x_t[:, 0, 0, :])
             for e in range(2):
                 words = x_pairs[pair][:, e, :].bitcast(F32)
                 for u in range(2):
@@ -167,8 +167,8 @@ def tile_geometricmanifoldnetwork_pa_kernel(
                 h_rows[(b, c)] = h_lin
             acc = psum.tile([P, BLOCK], F32, tag="bank")
             if (b, c, t) == (0, 0, 0):
-                for n in range(2):
-                    warm_up(acc[:])
+                for n in range(8):
+                    warm_up(acc[:, 0:P])
             for g in range(PASSES):
                 nc.tensor.matmul_mx(
                     out=acc[:],
@@ -246,9 +246,15 @@ def tile_geometricmanifoldnetwork_pa_kernel(
                 norm2 = work.tile([P, 2], F32, tag="norm2")
                 norms[pair] = norm2
             squares = work.tile([P, OUT], BF16, tag="squares")
-            nc.scalar.activation(
-                out=squares[:], in_=v_rows[i][:], func=ACT.Square, accum_out=norms[pair][:, e : e + 1]
-            )
+            if i == ROW_TILES - 1:
+                nc.vector.scalar_tensor_tensor(
+                    out=squares[:], in0=v_rows[i][:], scalar=1.0, in1=v_rows[i][:], op0=ALU.mult,
+                    op1=ALU.mult, accum_out=norms[pair][:, e : e + 1],
+                )
+            else:
+                nc.scalar.activation(
+                    out=squares[:], in_=v_rows[i][:], func=ACT.Square, accum_out=norms[pair][:, e : e + 1]
+                )
             if e == 1:
                 above = work.tile([P, 2], F32, tag="above")
                 nc.scalar.activation(
@@ -335,8 +341,7 @@ def tile_geometricmanifoldnetwork_pa_kernel(
             multiply_w2(i, (1,))
             add_b2(i)
             row_norm(i)
-            if i == 5:
-                scale_and_store(4, "gpsimd")
-                scale_and_store(5, "gpsimd")
+        scale_and_store(4, "vector")
+        scale_and_store(5, "vector")
         scale_and_store(6, "vector")
         scale_and_store(7, "vector")

@@ -133,7 +133,7 @@ def tile_geometricmanifoldnetwork_pa_kernel(
             b, half = divmod(pair, TILES_IN_BLOCK // 2)
             x_t = psum.tile([P, 2, 2, P], F32, tag="bank")
             if g == 0:
-                for n in range((18, 0, 4, 0)[pair]):
+                for n in range((18, 0, 0, 8)[pair]):
                     warm_up(x_t[:, 0, 0, :])
             for e in range(2):
                 words = x_pairs[pair][:, e, :].bitcast(F32)
@@ -151,11 +151,12 @@ def tile_geometricmanifoldnetwork_pa_kernel(
                 in_=x_t[:].rearrange("p e u r -> p e r u"),
             )
 
-        def quantise_x(b, g):
+        def quantise_x(b, g, first=0, rows=BLOCK):
+            at = g * BLOCK + first
             nc.vector.quantize_mx(
-                out=x_codes[b][:, g * BLOCK : (g + 1) * BLOCK].bitcast(FP8X4),
-                scales=x_plane[b][:, g * BLOCK : (g + 1) * BLOCK],
-                in_=x_grouped[(b, g)][:],
+                out=x_codes[b][:, at : at + rows].bitcast(FP8X4),
+                scales=x_plane[b][:, at : at + rows],
+                in_=x_grouped[(b, g)][:, PACK * first : PACK * (first + rows)],
             )
 
         h_rows = {}
@@ -166,9 +167,6 @@ def tile_geometricmanifoldnetwork_pa_kernel(
                 h_lin = halves.tile([P, PACK, BLOCK], BF16, tag="h_lin")
                 h_rows[(b, c)] = h_lin
             acc = psum.tile([P, BLOCK], F32, tag="bank")
-            if (b, c, t) == (0, 0, 0):
-                for n in range(8):
-                    warm_up(acc[:, 0:P])
             for g in range(PASSES):
                 nc.tensor.matmul_mx(
                     out=acc[:],
@@ -287,10 +285,10 @@ def tile_geometricmanifoldnetwork_pa_kernel(
             for pair in range(2 * b, 2 * b + 2):
                 for g in range(PASSES):
                     transpose_x(pair, g)
-            if b == 0:
-                for g in range(PASSES):
-                    quantise_x(b, g)
-                    if g == 0:
+                if b == 0:
+                    for g in range(PASSES):
+                        quantise_x(b, g, (pair % 2) * BLOCK // 2, BLOCK // 2)
+                    if pair == 0:
                         sort_w1_scales(0)
         for c in range(PASSES):
             if c == 1:
@@ -320,11 +318,10 @@ def tile_geometricmanifoldnetwork_pa_kernel(
             multiply_w2(i, (0,))
         group_tile(1, 1, 0, half)
         group_tile(1, 1, half, half)
-        interleave_h(1, 1, half, half + P, P, on_scalar=True)
+        interleave_h(1, 1, half, half, half, on_scalar=True)
         add_b2(0)
         row_norm(0)
         interleave_h(1, 1, 0, 0, half)
-        interleave_h(1, 1, half, half, P)
         add_b2(1)
         row_norm(1)
         scale_and_store(0, "gpsimd")

@@ -26,6 +26,7 @@ BLOCKS = BATCH // BLOCK
 TILES_IN_BLOCK = BLOCK // P
 QUADRANTS = 4
 EPS = 1e-12
+WARM_UPS = ((9, 0), (2, 1), (2, 1), (1, 0))
 
 FLOPS = 2 * BATCH * (PASSES * K_PASS) * HIDDEN + 2 * BATCH * HIDDEN * OUT
 
@@ -45,7 +46,7 @@ def tile_geometricmanifoldnetwork_pa_kernel(
 
         w1_scales_raw = consts.tile([P, HIDDEN], U8, align_bytes=64)
         w2_scales = consts.tile([P, OUT], U8, align_bytes=64)
-        zeros = consts.tile([P, P], BF16)
+        zeros = consts.tile([P, 2 * P], BF16)
         nc.vector.memset(zeros[:], 0.0)
         nc.vector.memset(w1_scales_raw[:].bitcast(I32), 0)
         nc.vector.memset(w2_scales[:].bitcast(I32), 0)
@@ -70,7 +71,7 @@ def tile_geometricmanifoldnetwork_pa_kernel(
             x_pair = x_pool.tile([P, 2, PASSES * K_PASS], BF16)
             nc.sync.dma_start(
                 out=x_pair[:],
-                in_=x[2 * pair * P : 2 * (pair + 1) * P, :].rearrange("(e p) k -> p e k", e=2),
+                in_=x[2 * pair * P : 2 * (pair + 1) * P, :].rearrange("(p e) k -> p e k", e=2),
             )
             x_pairs.append(x_pair)
             if pair == 0:
@@ -79,10 +80,13 @@ def tile_geometricmanifoldnetwork_pa_kernel(
         w1_raw = []
         for c in range(PASSES):
             w1_part = consts.tile([P, PASSES, K_PASS], I32, align_bytes=64, name="w1_part%d" % c)
-            nc.sync.dma_start(
-                out=w1_part[:],
-                in_=w1_bytes[:, :, 4 * K_PASS * c : 4 * K_PASS * (c + 1)].bitcast(I32),
-            )
+            for passes in ((0, 1), (1, 2)) if c == 0 else ((0, 2),):
+                nc.sync.dma_start(
+                    out=w1_part[:, passes[0] : passes[1], :],
+                    in_=w1_bytes[
+                        :, passes[0] : passes[1], 4 * K_PASS * c : 4 * K_PASS * (c + 1)
+                    ].bitcast(I32),
+                )
             w1_raw.append(w1_part)
             if c == 0:
                 b1_bf = consts.tile([P, PASSES, PACK], BF16)
@@ -127,14 +131,13 @@ def tile_geometricmanifoldnetwork_pa_kernel(
             x_plane.append(plane)
 
         def warm_up(bank):
-            nc.tensor.matmul(bank, lhsT=zeros[:], rhs=zeros[:], start=True, stop=True)
+            nc.tensor.matmul(bank, lhsT=zeros[:, 0:P], rhs=zeros[:], start=True, stop=True)
 
         def transpose_x(pair, g):
             b, half = divmod(pair, TILES_IN_BLOCK // 2)
             x_t = psum.tile([P, 2, 2, P], F32, tag="bank")
-            if g == 0:
-                for n in range((18, 0, 0, 8)[pair]):
-                    warm_up(x_t[:, 0, 0, :])
+            for n in range(WARM_UPS[pair][g]):
+                warm_up(x_t[:, 0, :, :])
             for e in range(2):
                 words = x_pairs[pair][:, e, :].bitcast(F32)
                 for u in range(2):
@@ -279,7 +282,8 @@ def tile_geometricmanifoldnetwork_pa_kernel(
                     out=unit[:], in0=v_rows[i][:], scalar1=factor, scalar2=0.0, op0=ALU.mult,
                     op1=ALU.add,
                 )
-            nc.sync.dma_start(out=out[i * P : (i + 1) * P, :], in_=unit[:])
+            rows = out[2 * pair * P : 2 * (pair + 1) * P, :].rearrange("(p e) n -> p e n", e=2)
+            nc.sync.dma_start(out=rows[:, e, :], in_=unit[:])
 
         for b in range(BLOCKS):
             for pair in range(2 * b, 2 * b + 2):
@@ -288,11 +292,8 @@ def tile_geometricmanifoldnetwork_pa_kernel(
                 if b == 0:
                     for g in range(PASSES):
                         quantise_x(b, g, (pair % 2) * BLOCK // 2, BLOCK // 2)
-                    if pair == 0:
-                        sort_w1_scales(0)
+                    sort_w1_scales(pair)
         for c in range(PASSES):
-            if c == 1:
-                sort_w1_scales(1)
             for g in range(PASSES):
                 sort_w1_codes(c, g)
         for g in range(PASSES):
@@ -327,9 +328,9 @@ def tile_geometricmanifoldnetwork_pa_kernel(
         scale_and_store(0, "gpsimd")
         scale_and_store(1, "gpsimd")
         quantise_h(1, 1, 0, half)
+        quantise_h(1, 1, half, half)
         add_b2(2)
         row_norm(2)
-        quantise_h(1, 1, half, half)
         add_b2(3)
         row_norm(3)
         scale_and_store(2, "gpsimd")

@@ -26,7 +26,7 @@ BLOCKS = BATCH // BLOCK
 TILES_IN_BLOCK = BLOCK // P
 QUADRANTS = 4
 EPS = 1e-12
-WARM_UPS = ((9, 0), (2, 1), (2, 1), (1, 0))
+WARM_UPS = (18, 0, 0, 8)
 
 FLOPS = 2 * BATCH * (PASSES * K_PASS) * HIDDEN + 2 * BATCH * HIDDEN * OUT
 
@@ -46,7 +46,7 @@ def tile_geometricmanifoldnetwork_pa_kernel(
 
         w1_scales_raw = consts.tile([P, HIDDEN], U8, align_bytes=64)
         w2_scales = consts.tile([P, OUT], U8, align_bytes=64)
-        zeros = consts.tile([P, 2 * P], BF16)
+        zeros = consts.tile([P, P], BF16)
         nc.vector.memset(zeros[:], 0.0)
         nc.vector.memset(w1_scales_raw[:].bitcast(I32), 0)
         nc.vector.memset(w2_scales[:].bitcast(I32), 0)
@@ -131,13 +131,14 @@ def tile_geometricmanifoldnetwork_pa_kernel(
             x_plane.append(plane)
 
         def warm_up(bank):
-            nc.tensor.matmul(bank, lhsT=zeros[:, 0:P], rhs=zeros[:], start=True, stop=True)
+            nc.tensor.matmul(bank, lhsT=zeros[:], rhs=zeros[:], start=True, stop=True)
 
         def transpose_x(pair, g):
             b, half = divmod(pair, TILES_IN_BLOCK // 2)
             x_t = psum.tile([P, 2, 2, P], F32, tag="bank")
-            for n in range(WARM_UPS[pair][g]):
-                warm_up(x_t[:, 0, :, :])
+            if g == 0:
+                for n in range(WARM_UPS[pair]):
+                    warm_up(x_t[:, 0, 0, :])
             for e in range(2):
                 words = x_pairs[pair][:, e, :].bitcast(F32)
                 for u in range(2):
@@ -190,12 +191,16 @@ def tile_geometricmanifoldnetwork_pa_kernel(
             grouped = halves.tile([P, rows, PACK], BF16, align_bytes=64, name="h_grouped_%d%d%d" % (b, c, first), bufs=1)
             h_grouped[(b, c, first)] = grouped
 
-        def interleave_h(b, c, tile_first=0, first=0, rows=BLOCK, on_scalar=False):
+        def interleave_h(b, c, tile_first=0, first=0, rows=BLOCK, engine="vector"):
             at = first - tile_first
             dst = h_grouped[(b, c, tile_first)][:, at : at + rows, :]
             planes = h_rows[(b, c)][:, :, first : first + rows].rearrange("p t r -> p r t")
-            if on_scalar:
+            if engine == "scalar":
                 nc.scalar.copy(out=dst, in_=planes)
+            elif engine == "gpsimd":
+                nc.gpsimd.tensor_scalar(
+                    out=dst, in0=planes, scalar1=1.0, scalar2=0.0, op0=ALU.mult, op1=ALU.add
+                )
             else:
                 nc.vector.tensor_copy(out=dst, in_=planes)
 
@@ -319,17 +324,16 @@ def tile_geometricmanifoldnetwork_pa_kernel(
             multiply_w2(i, (0,))
         group_tile(1, 1, 0, half)
         group_tile(1, 1, half, half)
-        interleave_h(1, 1, half, half, half, on_scalar=True)
-        add_b2(0)
-        row_norm(0)
-        interleave_h(1, 1, 0, 0, half)
-        add_b2(1)
-        row_norm(1)
+        interleave_h(1, 1, 0, 0, half, "scalar")
+        interleave_h(1, 1, half, half, half, "gpsimd")
+        for i in range(2):
+            add_b2(i)
+            row_norm(i)
         scale_and_store(0, "gpsimd")
         scale_and_store(1, "gpsimd")
+        add_b2(2)
         quantise_h(1, 1, 0, half)
         quantise_h(1, 1, half, half)
-        add_b2(2)
         row_norm(2)
         add_b2(3)
         row_norm(3)

@@ -44,8 +44,8 @@ def tile_geometricmanifoldnetwork_pa_kernel(
         psum = ctx.enter_context(tc.psum_pool(name="psum", bufs=8))
         ctx.enter_context(tc.manual_schedule())
 
-        w1_scales_raw = consts.tile([P, HIDDEN], U8, align_bytes=64)
-        w2_scales = consts.tile([P, OUT], U8, align_bytes=64)
+        w1_scales_raw = consts.tile([P, HIDDEN], U8, align_bytes=256)
+        w2_scales = consts.tile([P, OUT], U8, align_bytes=256)
         zeros = consts.tile([P, P], BF16)
         nc.vector.memset(zeros[:], 0.0)
         nc.vector.memset(w1_scales_raw[:].bitcast(I32), 0)
@@ -79,7 +79,7 @@ def tile_geometricmanifoldnetwork_pa_kernel(
         w1_bytes = W1_words.rearrange("g p n t -> p g (n t)")
         w1_raw = []
         for c in range(PASSES):
-            w1_part = consts.tile([P, PASSES, K_PASS], I32, align_bytes=64, name="w1_part%d" % c)
+            w1_part = consts.tile([P, PASSES, K_PASS], I32, align_bytes=256, name="w1_part%d" % c)
             for passes in ((0, 1), (1, 2)) if c == 0 else ((0, 2),):
                 nc.sync.dma_start(
                     out=w1_part[:, passes[0] : passes[1], :],
@@ -96,7 +96,7 @@ def tile_geometricmanifoldnetwork_pa_kernel(
                 b1_cols = consts.tile([P, PASSES, PACK], F32)
                 nc.gpsimd.tensor_copy(out=b1_cols[:], in_=b1_bf[:])
         load_scales(w2_scales, W2_scales)
-        w2_words = consts.tile([P, PASSES, OUT], U32, align_bytes=64)
+        w2_words = consts.tile([P, PASSES, OUT], U32, align_bytes=256)
         nc.sync.dma_start(
             out=w2_words[:].bitcast(I32),
             in_=W2_words.rearrange("g p n t -> p g (n t)").bitcast(I32),
@@ -104,8 +104,8 @@ def tile_geometricmanifoldnetwork_pa_kernel(
         b2_spread = consts.tile([P, OUT], BF16)
         nc.sync.dma_start(out=b2_spread[:], in_=b2.partition_broadcast(P))
 
-        w1_codes = consts.tile([P, PASSES, PASSES, PACK, P], I32, align_bytes=64)
-        w1_plane = consts.tile([P, PASSES, PACK, P], U8, align_bytes=64)
+        w1_codes = consts.tile([P, PASSES, PASSES, PACK, P], I32, align_bytes=256)
+        w1_plane = consts.tile([P, PASSES, PACK, P], U8, align_bytes=256)
 
         def sort_w1_scales(c):
             nc.vector.tensor_copy(
@@ -125,8 +125,8 @@ def tile_geometricmanifoldnetwork_pa_kernel(
         x_codes = []
         x_plane = []
         for b in range(BLOCKS):
-            codes = blocks.tile([P, PASSES * BLOCK], U32, align_bytes=64, tag="x_codes")
-            plane = blocks.tile([P, PASSES * BLOCK], U8, align_bytes=64, tag="x_plane")
+            codes = blocks.tile([P, PASSES * BLOCK], U32, align_bytes=256, tag="x_codes")
+            plane = blocks.tile([P, PASSES * BLOCK], U8, align_bytes=256, tag="x_plane")
             x_codes.append(codes)
             x_plane.append(plane)
 
@@ -146,7 +146,7 @@ def tile_geometricmanifoldnetwork_pa_kernel(
                         x_t[:, e, u, :], words[:, 256 * g + u : 256 * (g + 1) : 2], identity[:]
                     )
             if half == 0:
-                grouped = halves.tile([P, BLOCK * PACK], BF16, align_bytes=64, tag="x_grouped")
+                grouped = halves.tile([P, BLOCK * PACK], BF16, align_bytes=256, tag="x_grouped")
                 x_grouped[(b, g)] = grouped
             nc.scalar.copy(
                 out=x_grouped[(b, g)][:, half * 2 * K_PASS : (half + 1) * 2 * K_PASS]
@@ -188,7 +188,7 @@ def tile_geometricmanifoldnetwork_pa_kernel(
         h_grouped = {}
 
         def group_tile(b, c, first=0, rows=BLOCK):
-            grouped = halves.tile([P, rows, PACK], BF16, align_bytes=64, name="h_grouped_%d%d%d" % (b, c, first), bufs=1)
+            grouped = halves.tile([P, rows, PACK], BF16, align_bytes=256, name="h_grouped_%d%d%d" % (b, c, first), bufs=1)
             h_grouped[(b, c, first)] = grouped
 
         def interleave_h(b, c, tile_first=0, first=0, rows=BLOCK, engine="vector"):
@@ -206,8 +206,8 @@ def tile_geometricmanifoldnetwork_pa_kernel(
 
         def quantise_h(b, c, first=0, rows=BLOCK):
             if first == 0:
-                codes = halves.tile([P, BLOCK], U32, align_bytes=64, tag="h_codes")
-                plane = halves.tile([P, BLOCK], U8, align_bytes=64, tag="h_plane")
+                codes = halves.tile([P, BLOCK], U32, align_bytes=256, tag="h_codes")
+                plane = halves.tile([P, BLOCK], U8, align_bytes=256, tag="h_plane")
                 h_mx[(b, c)] = (codes, plane)
             codes, plane = h_mx[(b, c)]
             nc.vector.quantize_mx(

@@ -246,31 +246,31 @@ def tile_geometricmanifoldnetwork_pa_kernel(
 
         norms = {}
 
-        def row_norm(i):
+        def square_rows(i):
             pair, e = divmod(i, 2)
             if e == 0:
                 norm2 = work.tile([P, 2], F32, tag="norm2")
                 norms[pair] = norm2
             squares = work.tile([P, OUT], BF16, tag="squares")
-            if i == ROW_TILES - 1:
-                nc.vector.scalar_tensor_tensor(
-                    out=squares[:], in0=v_rows[i][:], scalar=1.0, in1=v_rows[i][:], op0=ALU.mult,
-                    op1=ALU.mult, accum_out=norms[pair][:, e : e + 1],
-                )
-            else:
-                nc.scalar.activation(
-                    out=squares[:], in_=v_rows[i][:], func=ACT.Square, accum_out=norms[pair][:, e : e + 1]
-                )
-            if e == 1:
-                above = work.tile([P, 2], F32, tag="above")
-                nc.scalar.activation(
-                    out=above[:], in_=norms[pair][:], func=ACT.Relu, bias=minus_floor2[:, 0:1]
-                )
-                inverse = work.tile([P, 2], F32, tag="inverse")
-                nc.scalar.activation(
-                    out=inverse[:], in_=above[:], func=ACT.Abs_reciprocal_sqrt, bias=floor2[:, 0:1]
-                )
-                inverses[pair] = inverse
+            nc.scalar.activation(
+                out=squares[:], in_=v_rows[i][:], func=ACT.Square, accum_out=norms[pair][:, e : e + 1]
+            )
+
+        aboves = {}
+
+        def floor_norms(pair):
+            above = work.tile([P, 2], F32, tag="above")
+            nc.scalar.activation(
+                out=above[:], in_=norms[pair][:], func=ACT.Relu, bias=minus_floor2[:, 0:1]
+            )
+            aboves[pair] = above
+
+        def invert_norms(pair):
+            inverse = work.tile([P, 2], F32, tag="inverse")
+            nc.scalar.activation(
+                out=inverse[:], in_=aboves[pair][:], func=ACT.Abs_reciprocal_sqrt, bias=floor2[:, 0:1]
+            )
+            inverses[pair] = inverse
 
         def scale_and_store(i, engine):
             pair, e = divmod(i, 2)
@@ -324,26 +324,36 @@ def tile_geometricmanifoldnetwork_pa_kernel(
             multiply_w2(i, (0,))
         group_tile(1, 1, 0, half)
         group_tile(1, 1, half, half)
-        interleave_h(1, 1, 0, 0, half, "scalar")
+        interleave_h(1, 1, 0, 0, P, "scalar")
+        interleave_h(1, 1, 0, P, half - P, "gpsimd")
         interleave_h(1, 1, half, half, half, "gpsimd")
         for i in range(2):
             add_b2(i)
-            row_norm(i)
+            square_rows(i)
+        floor_norms(0)
+        invert_norms(0)
         scale_and_store(0, "gpsimd")
         scale_and_store(1, "gpsimd")
-        add_b2(2)
-        quantise_h(1, 1, 0, half)
-        quantise_h(1, 1, half, half)
-        row_norm(2)
-        add_b2(3)
-        row_norm(3)
+        for i in range(2, TILES_IN_BLOCK):
+            add_b2(i)
+            square_rows(i)
+        floor_norms(1)
+        invert_norms(1)
         scale_and_store(2, "gpsimd")
         scale_and_store(3, "gpsimd")
+        quantise_h(1, 1, 0, half)
+        quantise_h(1, 1, half, half)
         for i in range(TILES_IN_BLOCK, ROW_TILES):
             multiply_w2(i, (1,))
             add_b2(i)
-            row_norm(i)
+            square_rows(i)
+            if i == 5:
+                floor_norms(2)
+            if i == 6:
+                invert_norms(2)
         scale_and_store(4, "vector")
         scale_and_store(5, "vector")
+        floor_norms(3)
+        invert_norms(3)
         scale_and_store(6, "vector")
         scale_and_store(7, "vector")

from contextlib import ExitStack

import concourse.masks as masks
import concourse.mybir as mybir

F32 = mybir.dt.float32
BF16 = mybir.dt.bfloat16
I32 = mybir.dt.int32
U32 = mybir.dt.uint32
U8 = mybir.dt.uint8
FP8X4 = mybir.dt.float8_e4m3fn_x4
ALU = mybir.AluOpType
ACT = mybir.ActivationFunctionType

P = 128
BATCH = 1024
K_PASS = 512
PASSES = 2
PACK = 4
HIDDEN = 1024
OUT = 512
BANK = 512
ROW_TILES = BATCH // P
BLOCK = 512
BLOCKS = BATCH // BLOCK
TILES_IN_BLOCK = BLOCK // P
QUADRANTS = 4
EPS = 1e-12
WARM_UPS = (18, 0, 0, 8)

FLOPS = 2 * BATCH * (PASSES * K_PASS) * HIDDEN + 2 * BATCH * HIDDEN * OUT


def tile_geometricmanifoldnetwork_pa_kernel(
    tc, x, W1_words, W1_scales, b1, W2_words, W2_scales, b2, out
):
    nc = tc.nc
    with ExitStack() as ctx:
        consts = ctx.enter_context(tc.tile_pool(name="consts", bufs=1))
        x_pool = ctx.enter_context(tc.tile_pool(name="x_pool", bufs=ROW_TILES // 2))
        blocks = ctx.enter_context(tc.tile_pool(name="blocks", bufs=BLOCKS))
        halves = ctx.enter_context(tc.tile_pool(name="halves", bufs=BLOCKS * PASSES))
        work = ctx.enter_context(tc.tile_pool(name="work", bufs=ROW_TILES))
        psum = ctx.enter_context(tc.psum_pool(name="psum", bufs=8))
        ctx.enter_context(tc.manual_schedule())

        w1_scales_raw = consts.tile([P, HIDDEN], U8, align_bytes=256)
        w2_scales = consts.tile([P, OUT], U8, align_bytes=256)
        zeros = consts.tile([P, P], BF16)
        nc.vector.memset(zeros[:], 0.0)
        nc.vector.memset(w1_scales_raw[:].bitcast(I32), 0)
        nc.vector.memset(w2_scales[:].bitcast(I32), 0)
        floor2 = consts.tile([P, 1], F32)
        nc.vector.memset(floor2[:], EPS * EPS)
        minus_floor2 = consts.tile([P, 1], F32)
        nc.vector.memset(minus_floor2[:], -EPS * EPS)
        warm = consts.tile([P, 1], F32)
        nc.scalar.activation(out=warm[:], in_=floor2[:], func=ACT.Abs_reciprocal_sqrt)
        identity = consts.tile([P, P], F32)
        masks.make_identity(nc, identity[:])

        def load_scales(plane, scales):
            for q in range(QUADRANTS):
                nc.sync.dma_start(
                    out=plane[32 * q : 32 * q + 4 * PASSES, :].bitcast(I32),
                    in_=scales[:, 4 * q : 4 * q + 4, :].bitcast(I32),
                )

        x_pairs = []
        for pair in range(ROW_TILES // 2):
            x_pair = x_pool.tile([P, 2, PASSES * K_PASS], BF16)
            nc.sync.dma_start(
                out=x_pair[:],
                in_=x[2 * pair * P : 2 * (pair + 1) * P, :].rearrange("(p e) k -> p e k", e=2),
            )
            x_pairs.append(x_pair)
            if pair == 0:
                load_scales(w1_scales_raw, W1_scales)
        w1_bytes = W1_words.rearrange("g p n t -> p g (n t)")
        w1_raw = []
        for c in range(PASSES):
            w1_part = consts.tile([P, PASSES, K_PASS], I32, align_bytes=256, name="w1_part%d" % c)
            for passes in ((0, 1), (1, 2)) if c == 0 else ((0, 2),):
                nc.sync.dma_start(
                    out=w1_part[:, passes[0] : passes[1], :],
                    in_=w1_bytes[
                        :, passes[0] : passes[1], 4 * K_PASS * c : 4 * K_PASS * (c + 1)
                    ].bitcast(I32),
                )
            w1_raw.append(w1_part)
            if c == 0:
                b1_bf = consts.tile([P, PASSES, PACK], BF16)
                nc.sync.dma_start(
                    out=b1_bf[:], in_=b1.rearrange("(c p t) -> p c t", c=PASSES, t=PACK)
                )
                b1_cols = consts.tile([P, PASSES, PACK], F32)
                nc.gpsimd.tensor_copy(out=b1_cols[:], in_=b1_bf[:])
        load_scales(w2_scales, W2_scales)
        w2_words = consts.tile([P, PASSES, OUT], U32, align_bytes=256)
        nc.sync.dma_start(
            out=w2_words[:].bitcast(I32),
            in_=W2_words.rearrange("g p n t -> p g (n t)").bitcast(I32),
        )
        b2_spread = consts.tile([P, OUT], BF16)
        nc.sync.dma_start(out=b2_spread[:], in_=b2.partition_broadcast(P))

        w1_codes = consts.tile([P, PASSES, PASSES, PACK, P], I32, align_bytes=256)
        w1_plane = consts.tile([P, PASSES, PACK, P], U8, align_bytes=256)

        def sort_w1_scales(c):
            nc.vector.tensor_copy(
                out=w1_plane[:, c, :, :],
                in_=w1_scales_raw[:, c * K_PASS : (c + 1) * K_PASS].rearrange(
                    "p (m t) -> p t m", t=PACK
                ),
            )

        def sort_w1_codes(c, g):
            nc.vector.tensor_copy(
                out=w1_codes[:, c, g, :, :].rearrange("p t m -> p m t"),
                in_=w1_raw[c][:, g, :].rearrange("p (m t) -> p m t", t=PACK),
            )

        x_grouped = {}
        x_codes = []
        x_plane = []
        for b in range(BLOCKS):
            codes = blocks.tile([P, PASSES * BLOCK], U32, align_bytes=256, tag="x_codes")
            plane = blocks.tile([P, PASSES * BLOCK], U8, align_bytes=256, tag="x_plane")
            x_codes.append(codes)
            x_plane.append(plane)

        def warm_up(bank):
            nc.tensor.matmul(bank, lhsT=zeros[:], rhs=zeros[:], start=True, stop=True)

        def transpose_x(pair, g):
            b, half = divmod(pair, TILES_IN_BLOCK // 2)
            x_t = psum.tile([P, 2, 2, P], F32, tag="bank")
            if g == 0:
                for n in range(WARM_UPS[pair]):
                    warm_up(x_t[:, 0, 0, :])
            for e in range(2):
                words = x_pairs[pair][:, e, :].bitcast(F32)
                for u in range(2):
                    nc.tensor.transpose(
                        x_t[:, e, u, :], words[:, 256 * g + u : 256 * (g + 1) : 2], identity[:]
                    )
            if half == 0:
                grouped = halves.tile([P, BLOCK * PACK], BF16, align_bytes=256, tag="x_grouped")
                x_grouped[(b, g)] = grouped
            nc.scalar.copy(
                out=x_grouped[(b, g)][:, half * 2 * K_PASS : (half + 1) * 2 * K_PASS]
                .bitcast(F32)
                .rearrange("p (e r u) -> p e r u", e=2, u=2),
                in_=x_t[:].rearrange("p e u r -> p e r u"),
            )

        def quantise_x(b, g, first=0, rows=BLOCK):
            at = g * BLOCK + first
            nc.vector.quantize_mx(
                out=x_codes[b][:, at : at + rows].bitcast(FP8X4),
                scales=x_plane[b][:, at : at + rows],
                in_=x_grouped[(b, g)][:, PACK * first : PACK * (first + rows)],
            )

        h_rows = {}
        h_mx = {}

        def multiply_w1(b, c, t):
            if t == 0:
                h_lin = halves.tile([P, PACK, BLOCK], BF16, tag="h_lin")
                h_rows[(b, c)] = h_lin
            acc = psum.tile([P, BLOCK], F32, tag="bank")
            for g in range(PASSES):
                nc.tensor.matmul_mx(
                    out=acc[:],
                    lhsT=w1_codes[:, c, g, t, :].bitcast(FP8X4),
                    lhsT_scale=w1_plane[4 * g : P, c, t, :],
                    rhs=x_codes[b][:, g * BLOCK : (g + 1) * BLOCK].bitcast(FP8X4),
                    rhs_scale=x_plane[b][:, g * BLOCK : (g + 1) * BLOCK],
                    start=(g == 0),
                    stop=(g == PASSES - 1),
                )
            nc.scalar.activation(
                out=h_rows[(b, c)][:, t, :], in_=acc[:], func=ACT.Relu, bias=b1_cols[:, c, t : t + 1]
            )

        h_grouped = {}

        def group_tile(b, c, first=0, rows=BLOCK):
            grouped = halves.tile([P, rows, PACK], BF16, align_bytes=256, name="h_grouped_%d%d%d" % (b, c, first), bufs=1)
            h_grouped[(b, c, first)] = grouped

        def interleave_h(b, c, tile_first=0, first=0, rows=BLOCK, engine="vector"):
            at = first - tile_first
            dst = h_grouped[(b, c, tile_first)][:, at : at + rows, :]
            planes = h_rows[(b, c)][:, :, first : first + rows].rearrange("p t r -> p r t")
            if engine == "scalar":
                nc.scalar.copy(out=dst, in_=planes)
            elif engine == "gpsimd":
                nc.gpsimd.tensor_scalar(
                    out=dst, in0=planes, scalar1=1.0, scalar2=0.0, op0=ALU.mult, op1=ALU.add
                )
            else:
                nc.vector.tensor_copy(out=dst, in_=planes)

        def quantise_h(b, c, first=0, rows=BLOCK):
            if first == 0:
                codes = halves.tile([P, BLOCK], U32, align_bytes=256, tag="h_codes")
                plane = halves.tile([P, BLOCK], U8, align_bytes=256, tag="h_plane")
                h_mx[(b, c)] = (codes, plane)
            codes, plane = h_mx[(b, c)]
            nc.vector.quantize_mx(
                out=codes[:, first : first + rows].bitcast(FP8X4),
                scales=plane[:, first : first + rows],
                in_=h_grouped[(b, c, first)][:].rearrange("p r t -> p (r t)"),
            )

        v_acc = {}
        v_rows = {}

        def multiply_w2(i, passes):
            b, j = divmod(i, TILES_IN_BLOCK)
            if 0 in passes:
                acc = psum.tile([P, OUT], F32, tag="bank")
                v_acc[i] = acc
            acc = v_acc[i]
            for c in passes:
                codes, plane = h_mx[(b, c)]
                nc.tensor.matmul_mx(
                    out=acc[:],
                    lhsT=codes[:, j * P : (j + 1) * P].bitcast(FP8X4),
                    lhsT_scale=plane[:, j * P : (j + 1) * P],
                    rhs=w2_words[:, c, :].bitcast(FP8X4),
                    rhs_scale=w2_scales[4 * c : P, :],
                    start=(c == 0),
                    stop=(c == PASSES - 1),
                )

        def add_b2(i):
            v = work.tile([P, OUT], F32, tag="v")
            nc.vector.tensor_tensor(out=v[:], in0=v_acc[i][:], in1=b2_spread[:], op=ALU.add)
            v_rows[i] = v

        inverses = {}

        norms = {}

        def square_rows(i):
            pair, e = divmod(i, 2)
            if e == 0:
                norm2 = work.tile([P, 2], F32, tag="norm2")
                norms[pair] = norm2
            squares = work.tile([P, OUT], BF16, tag="squares")
            nc.scalar.activation(
                out=squares[:], in_=v_rows[i][:], func=ACT.Square, accum_out=norms[pair][:, e : e + 1]
            )

        aboves = {}

        def floor_norms(pair):
            above = work.tile([P, 2], F32, tag="above")
            nc.scalar.activation(
                out=above[:], in_=norms[pair][:], func=ACT.Relu, bias=minus_floor2[:, 0:1]
            )
            aboves[pair] = above

        def invert_norms(pair):
            inverse = work.tile([P, 2], F32, tag="inverse")
            nc.scalar.activation(
                out=inverse[:], in_=aboves[pair][:], func=ACT.Abs_reciprocal_sqrt, bias=floor2[:, 0:1]
            )
            inverses[pair] = inverse

        def scale_and_store(i, engine):
            pair, e = divmod(i, 2)
            factor = inverses[pair][:, e : e + 1]
            unit = work.tile([P, OUT], F32, tag="unit")
            if engine == "scalar":
                nc.scalar.activation(out=unit[:], in_=v_rows[i][:], func=ACT.Copy, scale=factor)
            elif engine == "vector":
                nc.vector.tensor_scalar(
                    out=unit[:], in0=v_rows[i][:], scalar1=factor, scalar2=None, op0=ALU.mult
                )
            else:
                nc.gpsimd.tensor_scalar(
                    out=unit[:], in0=v_rows[i][:], scalar1=factor, scalar2=0.0, op0=ALU.mult,
                    op1=ALU.add,
                )
            rows = out[2 * pair * P : 2 * (pair + 1) * P, :].rearrange("(p e) n -> p e n", e=2)
            nc.sync.dma_start(out=rows[:, e, :], in_=unit[:])

        for b in range(BLOCKS):
            for pair in range(2 * b, 2 * b + 2):
                for g in range(PASSES):
                    transpose_x(pair, g)
                if b == 0:
                    for g in range(PASSES):
                        quantise_x(b, g, (pair % 2) * BLOCK // 2, BLOCK // 2)
                    sort_w1_scales(pair)
        for c in range(PASSES):
            for g in range(PASSES):
                sort_w1_codes(c, g)
        for g in range(PASSES):
            quantise_x(1, g)

        half = BLOCK // 2
        for c in range(PASSES):
            for t in range(PACK):
                multiply_w1(0, c, t)
            group_tile(0, c)
            interleave_h(0, c)
            quantise_h(0, c)
        for t in range(PACK):
            multiply_w1(1, 0, t)
        group_tile(1, 0)
        interleave_h(1, 0)
        for t in range(PACK):
            multiply_w1(1, 1, t)
        quantise_h(1, 0)
        for i in range(TILES_IN_BLOCK):
            multiply_w2(i, (0, 1))
        for i in range(TILES_IN_BLOCK, ROW_TILES):
            multiply_w2(i, (0,))
        group_tile(1, 1, 0, half)
        group_tile(1, 1, half, half)
        interleave_h(1, 1, 0, 0, P, "scalar")
        interleave_h(1, 1, 0, P, half - P, "gpsimd")
        interleave_h(1, 1, half, half, half, "gpsimd")
        for i in range(2):
            add_b2(i)
            square_rows(i)
        floor_norms(0)
        invert_norms(0)
        scale_and_store(0, "gpsimd")
        scale_and_store(1, "gpsimd")
        for i in range(2, TILES_IN_BLOCK):
            add_b2(i)
            square_rows(i)
        floor_norms(1)
        invert_norms(1)
        scale_and_store(2, "gpsimd")
        scale_and_store(3, "gpsimd")
        quantise_h(1, 1, 0, half)
        quantise_h(1, 1, half, half)
        for i in range(TILES_IN_BLOCK, ROW_TILES):
            multiply_w2(i, (1,))
            add_b2(i)
            square_rows(i)
            if i == 5:
                floor_norms(2)
            if i == 6:
                invert_norms(2)
        scale_and_store(4, "vector")
        scale_and_store(5, "vector")
        floor_norms(3)
        invert_norms(3)
        scale_and_store(6, "vector")
        scale_and_store(7, "vector")
